import numpy as np
import ml_dtypes


def mxq(x, axis, fmt="e4m3"):
    dtype, down = {"e4m3": (ml_dtypes.float8_e4m3fn, 7), "e5m2": (ml_dtypes.float8_e5m2, 14)}[fmt]
    v = np.moveaxis(np.asarray(x, np.float32).astype(ml_dtypes.bfloat16).astype(np.float64), axis, -1)
    blocks = v.reshape(v.shape[:-1] + (-1, 32))
    amax = np.abs(blocks).max(-1, keepdims=True)
    byte = np.maximum(np.where(amax > 0, np.frexp(amax)[1] - 1 + 127, 0) - down, 1)
    scale = np.exp2(byte - 127.0)
    codes = (blocks / scale).astype(np.float32).astype(dtype).astype(np.float64)
    return np.moveaxis((codes * scale).reshape(v.shape), -1, axis)


WIDE = False


def mx_kscale(k):
    if not WIDE:
        return np.ones(k)
    levels = np.array([10, -10, 5, -5, 0])
    a = np.random.permutation(np.resize(levels, k // 512 * 4)).reshape(k // 512, 4)
    idx = np.arange(k)
    return np.exp2(a[idx // 512, idx % 128 // 32])


BF16 = ml_dtypes.bfloat16


def bf(x):
    return np.asarray(x, np.float32).astype(BF16)


def f64(x):
    return np.asarray(x).astype(np.float64)


E2M1 = np.array([0.0, 0.5, 1.0, 1.5, 2.0, 3.0, 4.0, 6.0, -0.0, -0.5, -1.0, -1.5, -2.0, -3.0, -4.0, -6.0])


def pack_weight(w, fmt):
    k, n = w.shape
    w = f64(bf(w)).reshape(k // 32, 32, n)
    amax = np.abs(w).max(1)
    if fmt == "e4m3":
        byte = np.frexp(amax)[1] - 1 + 127 - 7
    else:
        mant, ex = np.frexp(amax / 6.0)
        byte = np.where(mant > 0.5, ex, ex - 1) + 127
    byte = np.clip(np.where(amax > 0, byte, 1), 1, 254)
    scaled = (w * np.exp2(127.0 - byte)[:, None, :]).reshape(k, n).astype(np.float32)
    by_word = np.ascontiguousarray(scaled.reshape(k // 512, 128, 4, n).transpose(0, 1, 3, 2))
    if fmt == "e4m3":
        words = by_word.astype(ml_dtypes.float8_e4m3fn).view(np.uint8)
    else:
        c = by_word.astype(ml_dtypes.float4_e2m1fn).view(np.uint8) & 0xF
        words = c[..., 0::2] | (c[..., 1::2] << 4)
    return np.ascontiguousarray(words), np.ascontiguousarray(byte.astype(np.uint8).reshape(k // 512, 16, n))


def unpack_weight(words, scales, fmt):
    g, p, n, _ = words.shape
    if fmt == "e4m3":
        vals = np.ascontiguousarray(words).view(ml_dtypes.float8_e4m3fn).astype(np.float64)
    else:
        nib = np.empty((g, p, n, 4), np.uint8)
        nib[..., 0::2] = words & 0xF
        nib[..., 1::2] = words >> 4
        vals = E2M1[nib]
    vals = vals * np.repeat(np.exp2(scales.astype(np.float64) - 127.0), 8, axis=1)[..., None]
    return vals.transpose(0, 1, 3, 2).reshape(g * 512, n)


B, S, HIDDEN, H, KV, D, SEC_T, SEC_H, SEC_W, PAD = 1, 1024, 2048, 16, 2, 128, 16, 24, 24, 256
SECTIONS = (SEC_T, SEC_H, SEC_W)
VALID = S - PAD
FMT = "e4m3"


def rotate_half(t):
    t1, t2 = np.split(t, 2, axis=-1)
    return np.concatenate((-t2, t1), axis=-1)


def reorder(t):
    chunks = []
    idx = 0
    for i in range(2 * len(SECTIONS)):
        sec = SECTIONS[i % len(SECTIONS)]
        chunks.append(t[i % len(SECTIONS), ..., idx:idx + sec])
        idx += sec
    return np.concatenate(chunks, axis=-1)


def setup_inputs():
    sc = mx_kscale(HIDDEN)
    w = 1.0 / np.sqrt(HIDDEN)
    ang = np.random.uniform(0.0, 2.0 * np.pi, (len(SECTIONS), B, S, D))
    mask = (np.arange(S)[None, :] < VALID) * np.ones((B, 1))
    x = bf(np.random.standard_normal((B, S, HIDDEN)) * sc)
    Wq_words, Wq_scales = pack_weight(np.random.standard_normal((HIDDEN, H * D)) * w / sc[:, None], FMT)
    bq = bf(np.random.standard_normal(H * D) * 0.2)
    Wk_words, Wk_scales = pack_weight(np.random.standard_normal((HIDDEN, KV * D)) * w / sc[:, None], FMT)
    bk = bf(np.random.standard_normal(KV * D) * 0.2)
    Wv_words, Wv_scales = pack_weight(np.random.standard_normal((HIDDEN, KV * D)) * w / sc[:, None], FMT)
    bv = bf(np.random.standard_normal(KV * D) * 0.2)
    return {"x": x,
            "cos": bf(np.cos(ang)), "sin": bf(np.sin(ang)), "mask": bf(mask),
            "Wq_words": Wq_words, "Wq_scales": Wq_scales, "bq": bq,
            "Wk_words": Wk_words, "Wk_scales": Wk_scales, "bk": bk,
            "Wv_words": Wv_words, "Wv_scales": Wv_scales, "bv": bv}


def reference(x, cos, sin, mask, Wq_words, Wq_scales, bq, Wk_words, Wk_scales, bk, Wv_words, Wv_scales, bv):
    xq = mxq(f64(x), 2, "e4m3")
    q = ((xq @ unpack_weight(Wq_words, Wq_scales, FMT)) + f64(bq)).reshape(B, S, H, D).transpose(0, 2, 1, 3)
    k = ((xq @ unpack_weight(Wk_words, Wk_scales, FMT)) + f64(bk)).reshape(B, S, KV, D).transpose(0, 2, 1, 3)
    v = ((xq @ unpack_weight(Wv_words, Wv_scales, FMT)) + f64(bv)).reshape(B, S, KV, D).transpose(0, 2, 1, 3)
    cos_e = reorder(f64(cos))[:, None]
    sin_e = reorder(f64(sin))[:, None]
    q = q * cos_e + rotate_half(q) * sin_e
    k = k * cos_e + rotate_half(k) * sin_e
    bm = f64(mask)[:, None, :, None]
    return q, k * bm, v * bm

@@ -1,0 +1,290 @@
+from contextlib import ExitStack
+
+import concourse.mybir as mybir
+from concourse.masks import make_identity
+
+F32 = mybir.dt.float32
+BF16 = mybir.dt.bfloat16
+I32 = mybir.dt.int32
+U32 = mybir.dt.uint32
+U8 = mybir.dt.uint8
+FP8X4 = mybir.dt.float8_e4m3fn_x4
+MULT = mybir.AluOpType.mult
+ADD = mybir.AluOpType.add
+IDENTITY = mybir.ActivationFunctionType.Identity
+
+P = 128
+PACK = 4
+TOKENS = 1024
+HIDDEN = 2048
+HEAD = 128
+HALF = HEAD // 2
+Q_HEADS = 16
+K_HEADS = 2
+V_HEADS = 2
+HEADS = Q_HEADS + K_HEADS + V_HEADS
+SECTIONS = (16, 24, 24)
+
+PASSES = HIDDEN // (P * PACK)
+WORDS_PER_PASS = P * PACK // 2
+TILES = TOKENS // P
+GROUP_TILES = 4
+GROUP_TOKENS = GROUP_TILES * P
+GROUPS = TILES // GROUP_TILES
+Q_CHUNK = 512
+
+UNITS_PER_ROUND = 2
+LATE_BANKS_PER_ROUND = 2
+
+FLOPS = 2 * TOKENS * HIDDEN * HEADS * HEAD
+BYTES = (
+    2 * TOKENS * HIDDEN
+    + 2 * 2 * TOKENS * HEAD
+    + 2 * TOKENS
+    + HIDDEN * HEADS * HEAD
+    + HIDDEN // 32 * HEADS * HEAD
+    + 2 * HEADS * HEAD
+    + 4 * TOKENS * HEADS * HEAD
+)
+
+
+def tile_multiheadattention_pa_kernel(
+    tc,
+    x,
+    cos,
+    sin,
+    mask,
+    Wq_words,
+    Wq_scales,
+    bq,
+    Wk_words,
+    Wk_scales,
+    bk,
+    Wv_words,
+    Wv_scales,
+    bv,
+    out_0,
+    out_1,
+    out_2,
+):
+    nc = tc.nc
+    with ExitStack() as ctx:
+        keep = ctx.enter_context(tc.tile_pool(name="keep", bufs=1))
+        stage = ctx.enter_context(tc.tile_pool(name="stage", bufs=2 * LATE_BANKS_PER_ROUND))
+        turned = ctx.enter_context(tc.tile_pool(name="turned", bufs=UNITS_PER_ROUND + 2))
+        halves = ctx.enter_context(tc.tile_pool(name="halves", bufs=3))
+        results = ctx.enter_context(tc.tile_pool(name="results", bufs=12))
+        sums = ctx.enter_context(tc.psum_pool(name="sums", bufs=2))
+        banks = ctx.enter_context(tc.psum_pool(name="banks", bufs=6))
+        ctx.enter_context(tc.manual_schedule())
+
+        ident = keep.tile([P, P], F32)
+        x_sb = keep.tile([P, TILES, HIDDEN], BF16)
+        w_words = keep.tile([P, PASSES, HEADS * HEAD], U32, align_bytes=64)
+        w_planes = keep.tile([P, HEADS * HEAD], U8, align_bytes=64)
+        x_codes = keep.tile([P, GROUPS, PASSES, GROUP_TOKENS], U32, align_bytes=64)
+        x_planes = keep.tile([P, GROUPS, PASSES, GROUP_TOKENS], U8, align_bytes=64)
+        bias_rows = keep.tile([P, HEAD], BF16)
+        bias_rows_f32 = keep.tile([P, HEAD], F32)
+        bias_cols = keep.tile([P, P], F32)
+        mask_sb = keep.tile([P, TILES], BF16)
+        raw_cos = keep.tile([P, len(SECTIONS), TILES, HEAD], BF16)
+        raw_sin = keep.tile([P, len(SECTIONS), TILES, HEAD], BF16)
+        rope_q = keep.tile([P, 2, TILES, HEAD], F32)
+        rope_k = keep.tile([P, 2, TILES, HEAD], F32)
+
+        make_identity(nc, ident[:])
+        nc.vector.memset(w_planes[:].bitcast(I32), 0)
+        nc.vector.memset(bias_rows[:], 0.0)
+
+        nc.scalar.dma_start(out=bias_rows[0:Q_HEADS, :], in_=bq.rearrange("(h d) -> h d", d=HEAD))
+        nc.scalar.dma_start(
+            out=bias_rows[Q_HEADS : Q_HEADS + K_HEADS, :], in_=bk.rearrange("(h d) -> h d", d=HEAD)
+        )
+        nc.scalar.dma_start(
+            out=bias_rows[Q_HEADS + K_HEADS : HEADS, :], in_=bv.rearrange("(h d) -> h d", d=HEAD)
+        )
+        nc.scalar.dma_start(out=mask_sb[:], in_=mask[0].rearrange("(p j) -> p j", j=TILES))
+
+        x_rows = x[0].rearrange("(p j) k -> p j k", j=TILES)
+
+        def load_x(j):
+            nc.sync.dma_start(out=x_sb[:, j, :], in_=x_rows[:, j, :])
+
+        def load_scales(scales, first_head, heads):
+            cols = slice(HEAD * first_head, HEAD * (first_head + heads))
+            for quadrant in range(4):
+                nc.sync.dma_start(
+                    out=w_planes[32 * quadrant : 32 * quadrant + 16, cols].bitcast(I32),
+                    in_=scales[:, 4 * quadrant : 4 * quadrant + 4, :].bitcast(I32),
+                )
+
+        def load_words(words, first_head, lo, hi):
+            first = HEAD * first_head
+            nc.sync.dma_start(
+                out=w_words[:, :, first + lo : first + hi].bitcast(I32),
+                in_=words.rearrange("g p n t -> p g (n t)")[:, :, PACK * lo : PACK * hi].bitcast(I32),
+            )
+
+        def load_table(raw, table):
+            nc.sync.dma_start(
+                out=raw[:].rearrange("p c j d -> p c (j d)"),
+                in_=table[:, 0].rearrange("c (p j) d -> p c (j d)", j=TILES),
+            )
+
+        for j in range(GROUP_TILES):
+            load_x(j)
+        load_scales(Wv_scales, Q_HEADS + K_HEADS, V_HEADS)
+        load_scales(Wk_scales, Q_HEADS, K_HEADS)
+        load_scales(Wq_scales, 0, Q_HEADS)
+        load_words(Wv_words, Q_HEADS + K_HEADS, 0, V_HEADS * HEAD)
+        load_words(Wk_words, Q_HEADS, 0, K_HEADS * HEAD)
+        load_table(raw_cos, cos)
+        load_table(raw_sin, sin)
+        load_words(Wq_words, 0, 0, Q_CHUNK)
+        load_words(Wq_words, 0, Q_CHUNK, 2 * Q_CHUNK)
+        for j in range(GROUP_TILES, TILES):
+            load_x(j)
+        load_words(Wq_words, 0, 2 * Q_CHUNK, 3 * Q_CHUNK)
+        load_words(Wq_words, 0, 3 * Q_CHUNK, 4 * Q_CHUNK)
+
+        def turn_x(j, pair):
+            bank = banks.tile([P, GROUP_TILES, P], F32, tag="bank")
+            words = x_sb[:, j, :].bitcast(F32)
+            for a in range(2):
+                first = WORDS_PER_PASS * (2 * pair + a)
+                for u in range(2):
+                    nc.tensor.transpose(
+                        out=bank[:, 2 * a + u, :],
+                        in_=words[:, first + u : first + WORDS_PER_PASS : 2],
+                        identity=ident[:],
+                    )
+            grouped = stage.tile([P, 2, P, PACK], BF16, tag="grouped", align_bytes=64)
+            nc.scalar.copy(
+                out=grouped[:]
+                .rearrange("p a s t -> p (a s t)")
+                .bitcast(F32)
+                .rearrange("p (a s u) -> p a s u", a=2, u=2),
+                in_=bank[:].rearrange("p (a u) s -> p a s u", u=2),
+            )
+            return grouped
+
+        def quantise_x(j, pair, grouped):
+            group, tile_in_group = divmod(j, GROUP_TILES)
+            cols = slice(P * tile_in_group, P * (tile_in_group + 1))
+            for a in range(2):
+                nc.vector.quantize_mx(
+                    out=x_codes[:, group, 2 * pair + a, cols].bitcast(FP8X4),
+                    scales=x_planes[:, group, 2 * pair + a, cols],
+                    in_=grouped[:, a].rearrange("p s t -> p (s t)"),
+                )
+
+        nc.vector.tensor_copy(out=bias_rows_f32[:], in_=bias_rows[:])
+        for j in range(GROUP_TILES):
+            for pair in range(PASSES // 2):
+                quantise_x(j, pair, turn_x(j, pair))
+
+        bias_bank = banks.tile([P, GROUP_TILES, P], F32, tag="bank")
+        nc.tensor.transpose(out=bias_bank[:, 0, :], in_=bias_rows_f32[:], identity=ident[:])
+        nc.vector.tensor_copy(out=bias_cols[:], in_=bias_bank[:, 0, :])
+
+        lo = 0
+        for i in range(2 * len(SECTIONS)):
+            c = i % len(SECTIONS)
+            hi = lo + SECTIONS[c]
+            nc.vector.tensor_copy(out=rope_q[:, 0, :, lo:hi], in_=raw_cos[:, c, :, lo:hi])
+            nc.vector.tensor_scalar_mul(
+                out=rope_q[:, 1, :, lo:hi],
+                in0=raw_sin[:, c, :, lo:hi],
+                scalar1=(-1.0 if lo < HALF else 1.0),
+            )
+            lo = hi
+        nc.vector.tensor_tensor(
+            out=rope_k[:],
+            in0=rope_q[:],
+            in1=mask_sb[:].unsqueeze(1).unsqueeze(3).to_broadcast([P, 2, TILES, HEAD]),
+            op=MULT,
+        )
+
+        heads = []
+        for h in range(V_HEADS):
+            heads.append((Q_HEADS + K_HEADS + h, None, out_2[0, h]))
+        for h in range(K_HEADS):
+            heads.append((Q_HEADS + h, rope_k, out_1[0, h]))
+        for h in range(Q_HEADS):
+            heads.append((h, rope_q, out_0[0, h]))
+        units = [(head, 0) for head in heads] + [(head, 1) for head in reversed(heads)]
+
+        def project(unit):
+            (head, table, dest), group = unit
+            cols = slice(HEAD * head, HEAD * (head + 1))
+            acc = sums.tile([P, GROUP_TOKENS], F32, tag="acc")
+            for g in range(PASSES):
+                nc.tensor.matmul_mx(
+                    out=acc[:],
+                    lhsT=w_words[:, g, cols].bitcast(FP8X4),
+                    lhsT_scale=w_planes[4 * g : P, cols],
+                    rhs=x_codes[:, group, g, :].bitcast(FP8X4),
+                    rhs_scale=x_planes[:, group, g, :],
+                    start=(g == 0),
+                    stop=(g == PASSES - 1),
+                )
+            biased = turned.tile([P, GROUP_TOKENS], F32, tag="biased")
+            nc.scalar.activation(
+                out=biased[:], in_=acc[:], func=IDENTITY, bias=bias_cols[:, head : head + 1], scale=1.0
+            )
+            return biased
+
+        def finish(unit, biased):
+            (head, table, dest), group = unit
+            bank = banks.tile([P, GROUP_TILES, HEAD], F32, tag="bank")
+            for t in range(GROUP_TILES):
+                nc.tensor.transpose(
+                    out=bank[:, t, :], in_=biased[:, P * t : P * (t + 1)], identity=ident[:]
+                )
+            tiles = slice(GROUP_TILES * group, GROUP_TILES * (group + 1))
+            result = results.tile([P, GROUP_TILES, HEAD], F32, tag="result")
+            if table is None:
+                nc.vector.tensor_tensor(
+                    out=result[:],
+                    in0=bank[:],
+                    in1=mask_sb[:, tiles].unsqueeze(2).to_broadcast([P, GROUP_TILES, HEAD]),
+                    op=MULT,
+                )
+            else:
+                partner = halves.tile([P, GROUP_TILES, HEAD], F32, tag="partner")
+                nc.vector.tensor_tensor(out=result[:], in0=bank[:], in1=table[:, 0, tiles, :], op=MULT)
+                nc.vector.tensor_tensor(
+                    out=partner[:, :, 0:HALF],
+                    in0=bank[:, :, HALF:HEAD],
+                    in1=table[:, 1, tiles, 0:HALF],
+                    op=MULT,
+                )
+                nc.vector.tensor_tensor(
+                    out=partner[:, :, HALF:HEAD],
+                    in0=bank[:, :, 0:HALF],
+                    in1=table[:, 1, tiles, HALF:HEAD],
+                    op=MULT,
+                )
+                nc.gpsimd.tensor_tensor(out=result[:], in0=result[:], in1=partner[:], op=ADD)
+            nc.sync.dma_start(
+                out=dest.rearrange("(p j) d -> p j d", j=TILES)[:, tiles, :], in_=result[:]
+            )
+
+        late_banks = [(j, pair) for j in range(GROUP_TILES, TILES) for pair in range(PASSES // 2)]
+        last_late_round = len(heads) // UNITS_PER_ROUND - 2
+        first_late_round = last_late_round + 1 - len(late_banks) // LATE_BANKS_PER_ROUND
+
+        biased_of = {0: project(units[0])}
+        for first in range(0, len(units), UNITS_PER_ROUND):
+            for i in range(first + 1, min(first + 1 + UNITS_PER_ROUND, len(units))):
+                biased_of[i] = project(units[i])
+            late = first // UNITS_PER_ROUND - first_late_round
+            due = []
+            if 0 <= late < len(late_banks) // LATE_BANKS_PER_ROUND:
+                due = late_banks[LATE_BANKS_PER_ROUND * late : LATE_BANKS_PER_ROUND * (late + 1)]
+            grouped_of = [turn_x(j, pair) for j, pair in due]
+            for i in range(first, first + UNITS_PER_ROUND):
+                finish(units[i], biased_of[i])
+            for (j, pair), grouped in zip(due, grouped_of):
+                quantise_x(j, pair, grouped)

@@ -12,6 +12,7 @@ FP8X4 = mybir.dt.float8_e4m3fn_x4
 MULT = mybir.AluOpType.mult
 ADD = mybir.AluOpType.add
 IDENTITY = mybir.ActivationFunctionType.Identity
+COPY = mybir.ActivationFunctionType.Copy
 
 P = 128
 PACK = 4
@@ -22,7 +23,8 @@ HALF = HEAD // 2
 Q_HEADS = 16
 K_HEADS = 2
 V_HEADS = 2
-HEADS = Q_HEADS + K_HEADS + V_HEADS
+KV_HEADS = K_HEADS + V_HEADS
+HEADS = Q_HEADS + KV_HEADS
 SECTIONS = (16, 24, 24)
 
 PASSES = HIDDEN // (P * PACK)
@@ -34,7 +36,6 @@ GROUPS = TILES // GROUP_TILES
 Q_CHUNK = 512
 
 UNITS_PER_ROUND = 2
-LATE_BANKS_PER_ROUND = 2
 
 FLOPS = 2 * TOKENS * HIDDEN * HEADS * HEAD
 BYTES = (
@@ -70,10 +71,11 @@ def tile_multiheadattention_pa_kernel(
     nc = tc.nc
     with ExitStack() as ctx:
         keep = ctx.enter_context(tc.tile_pool(name="keep", bufs=1))
-        stage = ctx.enter_context(tc.tile_pool(name="stage", bufs=2 * LATE_BANKS_PER_ROUND))
+        stage = ctx.enter_context(tc.tile_pool(name="stage", bufs=4))
         turned = ctx.enter_context(tc.tile_pool(name="turned", bufs=UNITS_PER_ROUND + 2))
         halves = ctx.enter_context(tc.tile_pool(name="halves", bufs=3))
         results = ctx.enter_context(tc.tile_pool(name="results", bufs=12))
+        kv_pool = ctx.enter_context(tc.tile_pool(name="kv", bufs=GROUP_TILES + 1))
         sums = ctx.enter_context(tc.psum_pool(name="sums", bufs=2))
         banks = ctx.enter_context(tc.psum_pool(name="banks", bufs=6))
         ctx.enter_context(tc.manual_schedule())
@@ -87,11 +89,12 @@ def tile_multiheadattention_pa_kernel(
         bias_rows = keep.tile([P, HEAD], BF16)
         bias_rows_f32 = keep.tile([P, HEAD], F32)
         bias_cols = keep.tile([P, P], F32)
-        mask_sb = keep.tile([P, TILES], BF16)
+        bias_kv = keep.tile([P, KV_HEADS, HEAD], F32)
+        mask_bf16 = keep.tile([P, TILES], BF16)
+        mask_sb = keep.tile([P, TILES], F32)
         raw_cos = keep.tile([P, len(SECTIONS), TILES, HEAD], BF16)
         raw_sin = keep.tile([P, len(SECTIONS), TILES, HEAD], BF16)
-        rope_q = keep.tile([P, 2, TILES, HEAD], F32)
-        rope_k = keep.tile([P, 2, TILES, HEAD], F32)
+        rope = keep.tile([P, 2, TILES, HEAD], F32)
 
         make_identity(nc, ident[:])
         nc.vector.memset(w_planes[:].bitcast(I32), 0)
@@ -104,7 +107,7 @@ def tile_multiheadattention_pa_kernel(
         nc.scalar.dma_start(
             out=bias_rows[Q_HEADS + K_HEADS : HEADS, :], in_=bv.rearrange("(h d) -> h d", d=HEAD)
         )
-        nc.scalar.dma_start(out=mask_sb[:], in_=mask[0].rearrange("(p j) -> p j", j=TILES))
+        nc.scalar.dma_start(out=mask_bf16[:], in_=mask[0].rearrange("(p j) -> p j", j=TILES))
 
         x_rows = x[0].rearrange("(p j) k -> p j k", j=TILES)
 
@@ -132,13 +135,15 @@ def tile_multiheadattention_pa_kernel(
                 in_=table[:, 0].rearrange("c (p j) d -> p c (j d)", j=TILES),
             )
 
-        for j in range(GROUP_TILES):
-            load_x(j)
-        load_scales(Wv_scales, Q_HEADS + K_HEADS, V_HEADS)
+        load_x(0)
+        load_x(1)
         load_scales(Wk_scales, Q_HEADS, K_HEADS)
+        load_scales(Wv_scales, Q_HEADS + K_HEADS, V_HEADS)
         load_scales(Wq_scales, 0, Q_HEADS)
-        load_words(Wv_words, Q_HEADS + K_HEADS, 0, V_HEADS * HEAD)
         load_words(Wk_words, Q_HEADS, 0, K_HEADS * HEAD)
+        load_words(Wv_words, Q_HEADS + K_HEADS, 0, V_HEADS * HEAD)
+        load_x(2)
+        load_x(3)
         load_table(raw_cos, cos)
         load_table(raw_sin, sin)
         load_words(Wq_words, 0, 0, Q_CHUNK)
@@ -148,75 +153,92 @@ def tile_multiheadattention_pa_kernel(
         load_words(Wq_words, 0, 2 * Q_CHUNK, 3 * Q_CHUNK)
         load_words(Wq_words, 0, 3 * Q_CHUNK, 4 * Q_CHUNK)
 
-        def turn_x(j, pair):
-            bank = banks.tile([P, GROUP_TILES, P], F32, tag="bank")
+        def turn_x(j):
             words = x_sb[:, j, :].bitcast(F32)
-            for a in range(2):
-                first = WORDS_PER_PASS * (2 * pair + a)
-                for u in range(2):
-                    nc.tensor.transpose(
-                        out=bank[:, 2 * a + u, :],
-                        in_=words[:, first + u : first + WORDS_PER_PASS : 2],
-                        identity=ident[:],
-                    )
-            grouped = stage.tile([P, 2, P, PACK], BF16, tag="grouped", align_bytes=64)
-            nc.scalar.copy(
-                out=grouped[:]
-                .rearrange("p a s t -> p (a s t)")
-                .bitcast(F32)
-                .rearrange("p (a s u) -> p a s u", a=2, u=2),
-                in_=bank[:].rearrange("p (a u) s -> p a s u", u=2),
-            )
-            return grouped
+            grouped_pairs = []
+            for pair in range(PASSES // 2):
+                bank = banks.tile([P, GROUP_TILES, P], F32, tag="bank")
+                for a in range(2):
+                    first = WORDS_PER_PASS * (2 * pair + a)
+                    for u in range(2):
+                        nc.tensor.transpose(
+                            out=bank[:, 2 * a + u, :],
+                            in_=words[:, first + u : first + WORDS_PER_PASS : 2],
+                            identity=ident[:],
+                        )
+                grouped = stage.tile([P, 2, P, PACK], BF16, tag="grouped", align_bytes=64)
+                nc.scalar.copy(
+                    out=grouped[:]
+                    .rearrange("p a s t -> p (a s t)")
+                    .bitcast(F32)
+                    .rearrange("p (a s u) -> p a s u", a=2, u=2),
+                    in_=bank[:].rearrange("p (a u) s -> p a s u", u=2),
+                )
+                grouped_pairs.append(grouped)
+            return grouped_pairs
 
-        def quantise_x(j, pair, grouped):
+        def quantise_x(j, grouped_pairs):
             group, tile_in_group = divmod(j, GROUP_TILES)
             cols = slice(P * tile_in_group, P * (tile_in_group + 1))
-            for a in range(2):
+            for g in range(PASSES):
                 nc.vector.quantize_mx(
-                    out=x_codes[:, group, 2 * pair + a, cols].bitcast(FP8X4),
-                    scales=x_planes[:, group, 2 * pair + a, cols],
-                    in_=grouped[:, a].rearrange("p s t -> p (s t)"),
+                    out=x_codes[:, group, g, cols].bitcast(FP8X4),
+                    scales=x_planes[:, group, g, cols],
+                    in_=grouped_pairs[g // 2][:, g % 2].rearrange("p s t -> p (s t)"),
                 )
 
-        nc.vector.tensor_copy(out=bias_rows_f32[:], in_=bias_rows[:])
-        for j in range(GROUP_TILES):
-            for pair in range(PASSES // 2):
-                quantise_x(j, pair, turn_x(j, pair))
+        def project_kv(j):
+            group, tile_in_group = divmod(j, GROUP_TILES)
+            rows = slice(P * tile_in_group, P * (tile_in_group + 1))
+            cols = slice(HEAD * Q_HEADS, HEAD * HEADS)
+            acc = sums.tile([P, KV_HEADS, HEAD], F32, tag="acc")
+            for g in range(PASSES):
+                nc.tensor.matmul_mx(
+                    out=acc[:].rearrange("p h d -> p (h d)"),
+                    lhsT=x_codes[:, group, g, rows].bitcast(FP8X4),
+                    lhsT_scale=x_planes[:, group, g, rows],
+                    rhs=w_words[:, g, cols].bitcast(FP8X4),
+                    rhs_scale=w_planes[4 * g : P, cols],
+                    start=(g == 0),
+                    stop=(g == PASSES - 1),
+                )
+            kv = kv_pool.tile([P, KV_HEADS, HEAD], F32, tag="kv")
+            nc.vector.tensor_tensor(out=kv[:], in0=acc[:], in1=bias_kv[:], op=ADD)
+            nc.scalar.activation(out=kv[:], in_=kv[:], func=COPY, scale=mask_sb[:, j : j + 1])
+            return kv
 
-        bias_bank = banks.tile([P, GROUP_TILES, P], F32, tag="bank")
-        nc.tensor.transpose(out=bias_bank[:, 0, :], in_=bias_rows_f32[:], identity=ident[:])
-        nc.vector.tensor_copy(out=bias_cols[:], in_=bias_bank[:, 0, :])
-
-        lo = 0
-        for i in range(2 * len(SECTIONS)):
-            c = i % len(SECTIONS)
-            hi = lo + SECTIONS[c]
-            nc.vector.tensor_copy(out=rope_q[:, 0, :, lo:hi], in_=raw_cos[:, c, :, lo:hi])
-            nc.vector.tensor_scalar_mul(
-                out=rope_q[:, 1, :, lo:hi],
-                in0=raw_sin[:, c, :, lo:hi],
-                scalar1=(-1.0 if lo < HALF else 1.0),
+        def finish_kv(j, kv):
+            k_out = kv_pool.tile([P, K_HEADS, HEAD], F32, tag="k_out")
+            k_partner = halves.tile([P, K_HEADS, HEAD], F32, tag="k_partner")
+            nc.vector.tensor_tensor(
+                out=k_out[:],
+                in0=kv[:, 0:K_HEADS, :],
+                in1=rope[:, 0, j, :].unsqueeze(1).to_broadcast([P, K_HEADS, HEAD]),
+                op=MULT,
             )
-            lo = hi
-        nc.vector.tensor_tensor(
-            out=rope_k[:],
-            in0=rope_q[:],
-            in1=mask_sb[:].unsqueeze(1).unsqueeze(3).to_broadcast([P, 2, TILES, HEAD]),
-            op=MULT,
-        )
+            nc.vector.tensor_tensor(
+                out=k_partner[:, :, 0:HALF],
+                in0=kv[:, 0:K_HEADS, HALF:HEAD],
+                in1=rope[:, 1, j, 0:HALF].unsqueeze(1).to_broadcast([P, K_HEADS, HALF]),
+                op=MULT,
+            )
+            nc.vector.tensor_tensor(
+                out=k_partner[:, :, HALF:HEAD],
+                in0=kv[:, 0:K_HEADS, 0:HALF],
+                in1=rope[:, 1, j, HALF:HEAD].unsqueeze(1).to_broadcast([P, K_HEADS, HALF]),
+                op=MULT,
+            )
+            nc.gpsimd.tensor_tensor(out=k_out[:], in0=k_out[:], in1=k_partner[:], op=ADD)
+            nc.sync.dma_start(
+                out=out_1[0].rearrange("h (p j) d -> p h j d", j=TILES)[:, :, j, :], in_=k_out[:]
+            )
+            nc.sync.dma_start(
+                out=out_2[0].rearrange("h (p j) d -> p h j d", j=TILES)[:, :, j, :],
+                in_=kv[:, K_HEADS:KV_HEADS, :],
+            )
 
-        heads = []
-        for h in range(V_HEADS):
-            heads.append((Q_HEADS + K_HEADS + h, None, out_2[0, h]))
-        for h in range(K_HEADS):
-            heads.append((Q_HEADS + h, rope_k, out_1[0, h]))
-        for h in range(Q_HEADS):
-            heads.append((h, rope_q, out_0[0, h]))
-        units = [(head, 0) for head in heads] + [(head, 1) for head in reversed(heads)]
-
-        def project(unit):
-            (head, table, dest), group = unit
+        def project_q(unit):
+            head, group = unit
             cols = slice(HEAD * head, HEAD * (head + 1))
             acc = sums.tile([P, GROUP_TOKENS], F32, tag="acc")
             for g in range(PASSES):
@@ -235,8 +257,8 @@ def tile_multiheadattention_pa_kernel(
             )
             return biased
 
-        def finish(unit, biased):
-            (head, table, dest), group = unit
+        def finish_q(unit, biased):
+            head, group = unit
             bank = banks.tile([P, GROUP_TILES, HEAD], F32, tag="bank")
             for t in range(GROUP_TILES):
                 nc.tensor.transpose(
@@ -244,47 +266,86 @@ def tile_multiheadattention_pa_kernel(
                 )
             tiles = slice(GROUP_TILES * group, GROUP_TILES * (group + 1))
             result = results.tile([P, GROUP_TILES, HEAD], F32, tag="result")
-            if table is None:
-                nc.vector.tensor_tensor(
-                    out=result[:],
-                    in0=bank[:],
-                    in1=mask_sb[:, tiles].unsqueeze(2).to_broadcast([P, GROUP_TILES, HEAD]),
-                    op=MULT,
-                )
-            else:
-                partner = halves.tile([P, GROUP_TILES, HEAD], F32, tag="partner")
-                nc.vector.tensor_tensor(out=result[:], in0=bank[:], in1=table[:, 0, tiles, :], op=MULT)
-                nc.vector.tensor_tensor(
-                    out=partner[:, :, 0:HALF],
-                    in0=bank[:, :, HALF:HEAD],
-                    in1=table[:, 1, tiles, 0:HALF],
-                    op=MULT,
-                )
-                nc.vector.tensor_tensor(
-                    out=partner[:, :, HALF:HEAD],
-                    in0=bank[:, :, 0:HALF],
-                    in1=table[:, 1, tiles, HALF:HEAD],
-                    op=MULT,
-                )
-                nc.gpsimd.tensor_tensor(out=result[:], in0=result[:], in1=partner[:], op=ADD)
+            partner = halves.tile([P, GROUP_TILES, HEAD], F32, tag="partner")
+            nc.vector.tensor_tensor(out=result[:], in0=bank[:], in1=rope[:, 0, tiles, :], op=MULT)
+            nc.vector.tensor_tensor(
+                out=partner[:, :, 0:HALF],
+                in0=bank[:, :, HALF:HEAD],
+                in1=rope[:, 1, tiles, 0:HALF],
+                op=MULT,
+            )
+            nc.vector.tensor_tensor(
+                out=partner[:, :, HALF:HEAD],
+                in0=bank[:, :, 0:HALF],
+                in1=rope[:, 1, tiles, HALF:HEAD],
+                op=MULT,
+            )
+            nc.gpsimd.tensor_tensor(out=result[:], in0=result[:], in1=partner[:], op=ADD)
             nc.sync.dma_start(
-                out=dest.rearrange("(p j) d -> p j d", j=TILES)[:, tiles, :], in_=result[:]
+                out=out_0[0, head].rearrange("(p j) d -> p j d", j=TILES)[:, tiles, :], in_=result[:]
             )
 
-        late_banks = [(j, pair) for j in range(GROUP_TILES, TILES) for pair in range(PASSES // 2)]
-        last_late_round = len(heads) // UNITS_PER_ROUND - 2
-        first_late_round = last_late_round + 1 - len(late_banks) // LATE_BANKS_PER_ROUND
+        quantise_x(0, turn_x(0))
+        quantise_x(1, turn_x(1))
 
-        biased_of = {0: project(units[0])}
-        for first in range(0, len(units), UNITS_PER_ROUND):
+        nc.vector.tensor_copy(out=bias_rows_f32[:], in_=bias_rows[:])
+        nc.vector.tensor_copy(out=mask_sb[:], in_=mask_bf16[:])
+        turned_bias = banks.tile([P, GROUP_TILES, P], F32, tag="bank")
+        nc.tensor.transpose(out=turned_bias[:, 0, :], in_=bias_rows_f32[:], identity=ident[:])
+        nc.vector.tensor_copy(out=bias_cols[:], in_=turned_bias[:, 0, :])
+        spread_bias = banks.tile([P, KV_HEADS, HEAD], F32, tag="bank")
+        for i in range(KV_HEADS):
+            nc.tensor.matmul(
+                out=spread_bias[:, i, :],
+                lhsT=ident[:, Q_HEADS + i : Q_HEADS + i + 1].to_broadcast([P, P]),
+                rhs=bias_rows_f32[:],
+                start=True,
+                stop=True,
+            )
+        nc.scalar.copy(out=bias_kv[:], in_=spread_bias[:])
+
+        kv_of = {0: project_kv(0)}
+        for j in range(2, GROUP_TILES):
+            quantise_x(j, turn_x(j))
+            kv_of[j - 1] = project_kv(j - 1)
+        kv_of[GROUP_TILES - 1] = project_kv(GROUP_TILES - 1)
+
+        lo = 0
+        for i in range(2 * len(SECTIONS)):
+            c = i % len(SECTIONS)
+            hi = lo + SECTIONS[c]
+            nc.vector.tensor_copy(out=rope[:, 0, :, lo:hi], in_=raw_cos[:, c, :, lo:hi])
+            nc.vector.tensor_scalar_mul(
+                out=rope[:, 1, :, lo:hi],
+                in0=raw_sin[:, c, :, lo:hi],
+                scalar1=(-1.0 if lo < HALF else 1.0),
+            )
+            lo = hi
+        for j in range(GROUP_TILES):
+            finish_kv(j, kv_of[j])
+
+        units = [(head, group) for group in range(GROUPS) for head in range(Q_HEADS)]
+        rounds_per_group = Q_HEADS // UNITS_PER_ROUND
+        first_late_round = rounds_per_group - 1 - GROUP_TILES
+        assert first_late_round >= 0
+
+        biased_of = {0: project_q(units[0])}
+        for r in range(len(units) // UNITS_PER_ROUND):
+            first = UNITS_PER_ROUND * r
+            x_tile = GROUP_TILES + r - first_late_round
+            kv_tile = x_tile - 1
+            turns_x = GROUP_TILES <= x_tile < TILES
+            projects_kv = GROUP_TILES <= kv_tile < TILES
+
             for i in range(first + 1, min(first + 1 + UNITS_PER_ROUND, len(units))):
-                biased_of[i] = project(units[i])
-            late = first // UNITS_PER_ROUND - first_late_round
-            due = []
-            if 0 <= late < len(late_banks) // LATE_BANKS_PER_ROUND:
-                due = late_banks[LATE_BANKS_PER_ROUND * late : LATE_BANKS_PER_ROUND * (late + 1)]
-            grouped_of = [turn_x(j, pair) for j, pair in due]
+                biased_of[i] = project_q(units[i])
+            if projects_kv:
+                kv_of[kv_tile] = project_kv(kv_tile)
+            if turns_x:
+                late_pairs = turn_x(x_tile)
             for i in range(first, first + UNITS_PER_ROUND):
-                finish(units[i], biased_of[i])
-            for (j, pair), grouped in zip(due, grouped_of):
-                quantise_x(j, pair, grouped)
+                finish_q(units[i], biased_of[i])
+            if projects_kv:
+                finish_kv(kv_tile, kv_of[kv_tile])
+            if turns_x:
+                quantise_x(x_tile, late_pairs)

@@ -12,7 +12,6 @@ FP8X4 = mybir.dt.float8_e4m3fn_x4
 MULT = mybir.AluOpType.mult
 ADD = mybir.AluOpType.add
 IDENTITY = mybir.ActivationFunctionType.Identity
-COPY = mybir.ActivationFunctionType.Copy
 
 P = 128
 PACK = 4
@@ -23,8 +22,7 @@ HALF = HEAD // 2
 Q_HEADS = 16
 K_HEADS = 2
 V_HEADS = 2
-KV_HEADS = K_HEADS + V_HEADS
-HEADS = Q_HEADS + KV_HEADS
+HEADS = Q_HEADS + K_HEADS + V_HEADS
 SECTIONS = (16, 24, 24)
 
 PASSES = HIDDEN // (P * PACK)
@@ -33,9 +31,9 @@ TILES = TOKENS // P
 GROUP_TILES = 4
 GROUP_TOKENS = GROUP_TILES * P
 GROUPS = TILES // GROUP_TILES
-Q_CHUNK = 512
+Q_CHUNK = 256
 
-UNITS_PER_ROUND = 2
+UNITS_PER_ROUND = 4
 
 FLOPS = 2 * TOKENS * HIDDEN * HEADS * HEAD
 BYTES = (
@@ -73,9 +71,8 @@ def tile_multiheadattention_pa_kernel(
         keep = ctx.enter_context(tc.tile_pool(name="keep", bufs=1))
         stage = ctx.enter_context(tc.tile_pool(name="stage", bufs=4))
         turned = ctx.enter_context(tc.tile_pool(name="turned", bufs=UNITS_PER_ROUND + 2))
-        halves = ctx.enter_context(tc.tile_pool(name="halves", bufs=3))
+        halves = ctx.enter_context(tc.tile_pool(name="halves", bufs=4))
         results = ctx.enter_context(tc.tile_pool(name="results", bufs=12))
-        kv_pool = ctx.enter_context(tc.tile_pool(name="kv", bufs=GROUP_TILES + 1))
         sums = ctx.enter_context(tc.psum_pool(name="sums", bufs=2))
         banks = ctx.enter_context(tc.psum_pool(name="banks", bufs=6))
         ctx.enter_context(tc.manual_schedule())
@@ -89,12 +86,11 @@ def tile_multiheadattention_pa_kernel(
         bias_rows = keep.tile([P, HEAD], BF16)
         bias_rows_f32 = keep.tile([P, HEAD], F32)
         bias_cols = keep.tile([P, P], F32)
-        bias_kv = keep.tile([P, KV_HEADS, HEAD], F32)
-        mask_bf16 = keep.tile([P, TILES], BF16)
-        mask_sb = keep.tile([P, TILES], F32)
+        mask_sb = keep.tile([P, TILES], BF16)
         raw_cos = keep.tile([P, len(SECTIONS), TILES, HEAD], BF16)
         raw_sin = keep.tile([P, len(SECTIONS), TILES, HEAD], BF16)
-        rope = keep.tile([P, 2, TILES, HEAD], F32)
+        rope_q = keep.tile([P, 2, TILES, HEAD], F32)
+        rope_k = keep.tile([P, 2, TILES, HEAD], F32)
 
         make_identity(nc, ident[:])
         nc.vector.memset(w_planes[:].bitcast(I32), 0)
@@ -107,7 +103,7 @@ def tile_multiheadattention_pa_kernel(
         nc.scalar.dma_start(
             out=bias_rows[Q_HEADS + K_HEADS : HEADS, :], in_=bv.rearrange("(h d) -> h d", d=HEAD)
         )
-        nc.scalar.dma_start(out=mask_bf16[:], in_=mask[0].rearrange("(p j) -> p j", j=TILES))
+        nc.scalar.dma_start(out=mask_sb[:], in_=mask[0].rearrange("(p j) -> p j", j=TILES))
 
         x_rows = x[0].rearrange("(p j) k -> p j k", j=TILES)
 
@@ -135,110 +131,97 @@ def tile_multiheadattention_pa_kernel(
                 in_=table[:, 0].rearrange("c (p j) d -> p c (j d)", j=TILES),
             )
 
-        load_x(0)
-        load_x(1)
+        for j in range(TILES):
+            load_x(j)
+        load_scales(Wq_scales, 0, Q_HEADS)
         load_scales(Wk_scales, Q_HEADS, K_HEADS)
         load_scales(Wv_scales, Q_HEADS + K_HEADS, V_HEADS)
-        load_scales(Wq_scales, 0, Q_HEADS)
-        load_words(Wk_words, Q_HEADS, 0, K_HEADS * HEAD)
-        load_words(Wv_words, Q_HEADS + K_HEADS, 0, V_HEADS * HEAD)
-        load_x(2)
-        load_x(3)
+        load_words(Wq_words, 0, 0, Q_CHUNK)
         load_table(raw_cos, cos)
         load_table(raw_sin, sin)
-        load_words(Wq_words, 0, 0, Q_CHUNK)
-        load_words(Wq_words, 0, Q_CHUNK, 2 * Q_CHUNK)
-        for j in range(GROUP_TILES, TILES):
-            load_x(j)
-        load_words(Wq_words, 0, 2 * Q_CHUNK, 3 * Q_CHUNK)
-        load_words(Wq_words, 0, 3 * Q_CHUNK, 4 * Q_CHUNK)
+        for lo in range(Q_CHUNK, Q_HEADS * HEAD, Q_CHUNK):
+            load_words(Wq_words, 0, lo, lo + Q_CHUNK)
+        load_words(Wk_words, Q_HEADS, 0, K_HEADS * HEAD)
+        load_words(Wv_words, Q_HEADS + K_HEADS, 0, V_HEADS * HEAD)
 
-        def turn_x(j):
+        def turn_x(j, pair):
+            bank = banks.tile([P, GROUP_TILES, P], F32, tag="bank")
             words = x_sb[:, j, :].bitcast(F32)
-            grouped_pairs = []
-            for pair in range(PASSES // 2):
-                bank = banks.tile([P, GROUP_TILES, P], F32, tag="bank")
-                for a in range(2):
-                    first = WORDS_PER_PASS * (2 * pair + a)
-                    for u in range(2):
-                        nc.tensor.transpose(
-                            out=bank[:, 2 * a + u, :],
-                            in_=words[:, first + u : first + WORDS_PER_PASS : 2],
-                            identity=ident[:],
-                        )
-                grouped = stage.tile([P, 2, P, PACK], BF16, tag="grouped", align_bytes=64)
-                nc.scalar.copy(
-                    out=grouped[:]
-                    .rearrange("p a s t -> p (a s t)")
-                    .bitcast(F32)
-                    .rearrange("p (a s u) -> p a s u", a=2, u=2),
-                    in_=bank[:].rearrange("p (a u) s -> p a s u", u=2),
-                )
-                grouped_pairs.append(grouped)
-            return grouped_pairs
+            for a in range(2):
+                first = WORDS_PER_PASS * (2 * pair + a)
+                for u in range(2):
+                    nc.tensor.transpose(
+                        out=bank[:, 2 * a + u, :],
+                        in_=words[:, first + u : first + WORDS_PER_PASS : 2],
+                        identity=ident[:],
+                    )
+            grouped = stage.tile([P, 2, P, PACK], BF16, tag="grouped", align_bytes=64)
+            grouped_words = (
+                grouped[:]
+                .rearrange("p a s t -> p (a s t)")
+                .bitcast(F32)
+                .rearrange("p (a s u) -> p a s u", a=2, u=2)
+            )
+            bank_words = bank[:].rearrange("p (a u) s -> p a s u", u=2)
+            if (2 * j + pair) % 4 == 3:
+                nc.vector.tensor_copy(out=grouped_words, in_=bank_words)
+            else:
+                nc.scalar.copy(out=grouped_words, in_=bank_words)
+            return grouped
 
-        def quantise_x(j, grouped_pairs):
+        def quantise_x(j, pair, grouped):
             group, tile_in_group = divmod(j, GROUP_TILES)
             cols = slice(P * tile_in_group, P * (tile_in_group + 1))
-            for g in range(PASSES):
+            for a in range(2):
                 nc.vector.quantize_mx(
-                    out=x_codes[:, group, g, cols].bitcast(FP8X4),
-                    scales=x_planes[:, group, g, cols],
-                    in_=grouped_pairs[g // 2][:, g % 2].rearrange("p s t -> p (s t)"),
+                    out=x_codes[:, group, 2 * pair + a, cols].bitcast(FP8X4),
+                    scales=x_planes[:, group, 2 * pair + a, cols],
+                    in_=grouped[:, a].rearrange("p s t -> p (s t)"),
                 )
 
-        def project_kv(j):
-            group, tile_in_group = divmod(j, GROUP_TILES)
-            rows = slice(P * tile_in_group, P * (tile_in_group + 1))
-            cols = slice(HEAD * Q_HEADS, HEAD * HEADS)
-            acc = sums.tile([P, KV_HEADS, HEAD], F32, tag="acc")
-            for g in range(PASSES):
-                nc.tensor.matmul_mx(
-                    out=acc[:].rearrange("p h d -> p (h d)"),
-                    lhsT=x_codes[:, group, g, rows].bitcast(FP8X4),
-                    lhsT_scale=x_planes[:, group, g, rows],
-                    rhs=w_words[:, g, cols].bitcast(FP8X4),
-                    rhs_scale=w_planes[4 * g : P, cols],
-                    start=(g == 0),
-                    stop=(g == PASSES - 1),
-                )
-            kv = kv_pool.tile([P, KV_HEADS, HEAD], F32, tag="kv")
-            nc.vector.tensor_tensor(out=kv[:], in0=acc[:], in1=bias_kv[:], op=ADD)
-            nc.scalar.activation(out=kv[:], in_=kv[:], func=COPY, scale=mask_sb[:, j : j + 1])
-            return kv
+        nc.vector.tensor_copy(out=bias_rows_f32[:], in_=bias_rows[:])
+        waiting = None
+        for j in range(TILES):
+            for pair in range(PASSES // 2):
+                grouped = turn_x(j, pair)
+                if waiting is not None:
+                    quantise_x(*waiting)
+                waiting = (j, pair, grouped)
+        quantise_x(*waiting)
 
-        def finish_kv(j, kv):
-            k_out = kv_pool.tile([P, K_HEADS, HEAD], F32, tag="k_out")
-            k_partner = halves.tile([P, K_HEADS, HEAD], F32, tag="k_partner")
-            nc.vector.tensor_tensor(
-                out=k_out[:],
-                in0=kv[:, 0:K_HEADS, :],
-                in1=rope[:, 0, j, :].unsqueeze(1).to_broadcast([P, K_HEADS, HEAD]),
-                op=MULT,
-            )
-            nc.vector.tensor_tensor(
-                out=k_partner[:, :, 0:HALF],
-                in0=kv[:, 0:K_HEADS, HALF:HEAD],
-                in1=rope[:, 1, j, 0:HALF].unsqueeze(1).to_broadcast([P, K_HEADS, HALF]),
-                op=MULT,
-            )
-            nc.vector.tensor_tensor(
-                out=k_partner[:, :, HALF:HEAD],
-                in0=kv[:, 0:K_HEADS, 0:HALF],
-                in1=rope[:, 1, j, HALF:HEAD].unsqueeze(1).to_broadcast([P, K_HEADS, HALF]),
-                op=MULT,
-            )
-            nc.gpsimd.tensor_tensor(out=k_out[:], in0=k_out[:], in1=k_partner[:], op=ADD)
-            nc.sync.dma_start(
-                out=out_1[0].rearrange("h (p j) d -> p h j d", j=TILES)[:, :, j, :], in_=k_out[:]
-            )
-            nc.sync.dma_start(
-                out=out_2[0].rearrange("h (p j) d -> p h j d", j=TILES)[:, :, j, :],
-                in_=kv[:, K_HEADS:KV_HEADS, :],
-            )
+        bias_bank = banks.tile([P, GROUP_TILES, P], F32, tag="bank")
+        nc.tensor.transpose(out=bias_bank[:, 0, :], in_=bias_rows_f32[:], identity=ident[:])
+        nc.vector.tensor_copy(out=bias_cols[:], in_=bias_bank[:, 0, :])
 
-        def project_q(unit):
-            head, group = unit
+        lo = 0
+        for i in range(2 * len(SECTIONS)):
+            c = i % len(SECTIONS)
+            hi = lo + SECTIONS[c]
+            nc.vector.tensor_copy(out=rope_q[:, 0, :, lo:hi], in_=raw_cos[:, c, :, lo:hi])
+            nc.gpsimd.tensor_scalar(
+                out=rope_q[:, 1, :, lo:hi],
+                in0=raw_sin[:, c, :, lo:hi],
+                scalar1=(-1.0 if lo < HALF else 1.0),
+                scalar2=0.0,
+                op0=MULT,
+                op1=ADD,
+            )
+            lo = hi
+        mask_of_row = mask_sb[:].unsqueeze(2).to_broadcast([P, TILES, HEAD])
+        nc.vector.tensor_tensor(out=rope_k[:, 0], in0=rope_q[:, 0], in1=mask_of_row, op=MULT)
+        nc.gpsimd.tensor_tensor(out=rope_k[:, 1], in0=rope_q[:, 1], in1=mask_of_row, op=MULT)
+
+        heads = []
+        for h in range(Q_HEADS):
+            heads.append((h, rope_q, out_0[0, h]))
+        for h in range(K_HEADS):
+            heads.append((Q_HEADS + h, rope_k, out_1[0, h]))
+        for h in range(V_HEADS):
+            heads.append((Q_HEADS + K_HEADS + h, None, out_2[0, h]))
+        units = [(head, group) for head in heads for group in range(GROUPS)]
+
+        def project(unit):
+            (head, table, dest), group = unit
             cols = slice(HEAD * head, HEAD * (head + 1))
             acc = sums.tile([P, GROUP_TOKENS], F32, tag="acc")
             for g in range(PASSES):
@@ -257,8 +240,8 @@ def tile_multiheadattention_pa_kernel(
             )
             return biased
 
-        def finish_q(unit, biased):
-            head, group = unit
+        def finish(unit, biased):
+            (head, table, dest), group = unit
             bank = banks.tile([P, GROUP_TILES, HEAD], F32, tag="bank")
             for t in range(GROUP_TILES):
                 nc.tensor.transpose(
@@ -266,86 +249,36 @@ def tile_multiheadattention_pa_kernel(
                 )
             tiles = slice(GROUP_TILES * group, GROUP_TILES * (group + 1))
             result = results.tile([P, GROUP_TILES, HEAD], F32, tag="result")
-            partner = halves.tile([P, GROUP_TILES, HEAD], F32, tag="partner")
-            nc.vector.tensor_tensor(out=result[:], in0=bank[:], in1=rope[:, 0, tiles, :], op=MULT)
-            nc.vector.tensor_tensor(
-                out=partner[:, :, 0:HALF],
-                in0=bank[:, :, HALF:HEAD],
-                in1=rope[:, 1, tiles, 0:HALF],
-                op=MULT,
-            )
-            nc.vector.tensor_tensor(
-                out=partner[:, :, HALF:HEAD],
-                in0=bank[:, :, 0:HALF],
-                in1=rope[:, 1, tiles, HALF:HEAD],
-                op=MULT,
-            )
-            nc.gpsimd.tensor_tensor(out=result[:], in0=result[:], in1=partner[:], op=ADD)
+            if table is None:
+                nc.vector.tensor_tensor(
+                    out=result[:],
+                    in0=bank[:],
+                    in1=mask_sb[:, tiles].unsqueeze(2).to_broadcast([P, GROUP_TILES, HEAD]),
+                    op=MULT,
+                )
+            else:
+                partner = halves.tile([P, GROUP_TILES, HEAD], F32, tag="partner")
+                nc.vector.tensor_tensor(out=result[:], in0=bank[:], in1=table[:, 0, tiles, :], op=MULT)
+                nc.vector.tensor_tensor(
+                    out=partner[:, :, 0:HALF],
+                    in0=bank[:, :, HALF:HEAD],
+                    in1=table[:, 1, tiles, 0:HALF],
+                    op=MULT,
+                )
+                nc.vector.tensor_tensor(
+                    out=partner[:, :, HALF:HEAD],
+                    in0=bank[:, :, 0:HALF],
+                    in1=table[:, 1, tiles, HALF:HEAD],
+                    op=MULT,
+                )
+                nc.gpsimd.tensor_tensor(out=result[:], in0=result[:], in1=partner[:], op=ADD)
             nc.sync.dma_start(
-                out=out_0[0, head].rearrange("(p j) d -> p j d", j=TILES)[:, tiles, :], in_=result[:]
+                out=dest.rearrange("(p j) d -> p j d", j=TILES)[:, tiles, :], in_=result[:]
             )
 
-        quantise_x(0, turn_x(0))
-        quantise_x(1, turn_x(1))
-
-        nc.vector.tensor_copy(out=bias_rows_f32[:], in_=bias_rows[:])
-        nc.vector.tensor_copy(out=mask_sb[:], in_=mask_bf16[:])
-        turned_bias = banks.tile([P, GROUP_TILES, P], F32, tag="bank")
-        nc.tensor.transpose(out=turned_bias[:, 0, :], in_=bias_rows_f32[:], identity=ident[:])
-        nc.vector.tensor_copy(out=bias_cols[:], in_=turned_bias[:, 0, :])
-        spread_bias = banks.tile([P, KV_HEADS, HEAD], F32, tag="bank")
-        for i in range(KV_HEADS):
-            nc.tensor.matmul(
-                out=spread_bias[:, i, :],
-                lhsT=ident[:, Q_HEADS + i : Q_HEADS + i + 1].to_broadcast([P, P]),
-                rhs=bias_rows_f32[:],
-                start=True,
-                stop=True,
-            )
-        nc.scalar.copy(out=bias_kv[:], in_=spread_bias[:])
-
-        kv_of = {0: project_kv(0)}
-        for j in range(2, GROUP_TILES):
-            quantise_x(j, turn_x(j))
-            kv_of[j - 1] = project_kv(j - 1)
-        kv_of[GROUP_TILES - 1] = project_kv(GROUP_TILES - 1)
-
-        lo = 0
-        for i in range(2 * len(SECTIONS)):
-            c = i % len(SECTIONS)
-            hi = lo + SECTIONS[c]
-            nc.vector.tensor_copy(out=rope[:, 0, :, lo:hi], in_=raw_cos[:, c, :, lo:hi])
-            nc.vector.tensor_scalar_mul(
-                out=rope[:, 1, :, lo:hi],
-                in0=raw_sin[:, c, :, lo:hi],
-                scalar1=(-1.0 if lo < HALF else 1.0),
-            )
-            lo = hi
-        for j in range(GROUP_TILES):
-            finish_kv(j, kv_of[j])
-
-        units = [(head, group) for group in range(GROUPS) for head in range(Q_HEADS)]
-        rounds_per_group = Q_HEADS // UNITS_PER_ROUND
-        first_late_round = rounds_per_group - 1 - GROUP_TILES
-        assert first_late_round >= 0
-
-        biased_of = {0: project_q(units[0])}
-        for r in range(len(units) // UNITS_PER_ROUND):
-            first = UNITS_PER_ROUND * r
-            x_tile = GROUP_TILES + r - first_late_round
-            kv_tile = x_tile - 1
-            turns_x = GROUP_TILES <= x_tile < TILES
-            projects_kv = GROUP_TILES <= kv_tile < TILES
-
+        biased_of = {0: project(units[0])}
+        for first in range(0, len(units), UNITS_PER_ROUND):
             for i in range(first + 1, min(first + 1 + UNITS_PER_ROUND, len(units))):
-                biased_of[i] = project_q(units[i])
-            if projects_kv:
-                kv_of[kv_tile] = project_kv(kv_tile)
-            if turns_x:
-                late_pairs = turn_x(x_tile)
+                biased_of[i] = project(units[i])
             for i in range(first, first + UNITS_PER_ROUND):
-                finish_q(units[i], biased_of[i])
-            if projects_kv:
-                finish_kv(kv_tile, kv_of[kv_tile])
-            if turns_x:
-                quantise_x(x_tile, late_pairs)
+                finish(units[i], biased_of[i])

@@ -73,8 +73,8 @@ def tile_multiheadattention_pa_kernel(
         turned = ctx.enter_context(tc.tile_pool(name="turned", bufs=UNITS_PER_ROUND + 2))
         halves = ctx.enter_context(tc.tile_pool(name="halves", bufs=4))
         results = ctx.enter_context(tc.tile_pool(name="results", bufs=12))
-        sums = ctx.enter_context(tc.psum_pool(name="sums", bufs=2))
-        banks = ctx.enter_context(tc.psum_pool(name="banks", bufs=6))
+        sums = ctx.enter_context(tc.psum_pool(name="sums", bufs=3))
+        banks = ctx.enter_context(tc.psum_pool(name="banks", bufs=5))
         ctx.enter_context(tc.manual_schedule())
 
         ident = keep.tile([P, P], F32)

@@ -33,7 +33,7 @@ GROUP_TOKENS = GROUP_TILES * P
 GROUPS = TILES // GROUP_TILES
 Q_CHUNK = 256
 
-UNITS_PER_ROUND = 4
+UNITS_PER_ROUND = 3
 
 FLOPS = 2 * TOKENS * HIDDEN * HEADS * HEAD
 BYTES = (
@@ -280,5 +280,5 @@ def tile_multiheadattention_pa_kernel(
         for first in range(0, len(units), UNITS_PER_ROUND):
             for i in range(first + 1, min(first + 1 + UNITS_PER_ROUND, len(units))):
                 biased_of[i] = project(units[i])
-            for i in range(first, first + UNITS_PER_ROUND):
+            for i in range(first, min(first + UNITS_PER_ROUND, len(units))):
                 finish(units[i], biased_of[i])

@@ -12,6 +12,7 @@ FP8X4 = mybir.dt.float8_e4m3fn_x4
 MULT = mybir.AluOpType.mult
 ADD = mybir.AluOpType.add
 IDENTITY = mybir.ActivationFunctionType.Identity
+COPY = mybir.ActivationFunctionType.Copy
 
 P = 128
 PACK = 4
@@ -87,6 +88,9 @@ def tile_multiheadattention_pa_kernel(
         bias_rows_f32 = keep.tile([P, HEAD], F32)
         bias_cols = keep.tile([P, P], F32)
         mask_sb = keep.tile([P, TILES], BF16)
+        mask_f32 = keep.tile([P, TILES], F32)
+        bv_masked = keep.tile([P, TILES, V_HEADS * HEAD], F32)
+        bv_rows = keep.tile([P, V_HEADS * HEAD], F32)
         raw_cos = keep.tile([P, len(SECTIONS), TILES, HEAD], BF16)
         raw_sin = keep.tile([P, len(SECTIONS), TILES, HEAD], BF16)
         rope_q = keep.tile([P, 2, TILES, HEAD], F32)
@@ -192,6 +196,23 @@ def tile_multiheadattention_pa_kernel(
         bias_bank = banks.tile([P, GROUP_TILES, P], F32, tag="bank")
         nc.tensor.transpose(out=bias_bank[:, 0, :], in_=bias_rows_f32[:], identity=ident[:])
         nc.vector.tensor_copy(out=bias_cols[:], in_=bias_bank[:, 0, :])
+        nc.vector.tensor_copy(out=mask_f32[:], in_=mask_sb[:])
+        bv_bank = banks.tile([P, GROUP_TILES, P], F32, tag="bank")
+        for h in range(V_HEADS):
+            column = Q_HEADS + K_HEADS + h
+            nc.tensor.transpose(
+                out=bv_bank[:, h, :],
+                in_=bias_cols[:, column : column + 1].to_broadcast([P, P]),
+                identity=ident[:],
+            )
+        nc.vector.tensor_copy(
+            out=bv_rows[:], in_=bv_bank[:, 0:V_HEADS, :].rearrange("p h d -> p (h d)")
+        )
+
+        def mask_bv(j):
+            nc.scalar.activation(
+                out=bv_masked[:, j, :], in_=bv_rows[:], func=COPY, scale=mask_f32[:, j : j + 1]
+            )
 
         lo = 0
         for i in range(2 * len(SECTIONS)):
@@ -216,8 +237,6 @@ def tile_multiheadattention_pa_kernel(
             heads.append((h, rope_q, out_0[0, h]))
         for h in range(K_HEADS):
             heads.append((Q_HEADS + h, rope_k, out_1[0, h]))
-        for h in range(V_HEADS):
-            heads.append((Q_HEADS + K_HEADS + h, None, out_2[0, h]))
         units = [(head, group) for head in heads for group in range(GROUPS)]
 
         def project(unit):
@@ -249,29 +268,21 @@ def tile_multiheadattention_pa_kernel(
                 )
             tiles = slice(GROUP_TILES * group, GROUP_TILES * (group + 1))
             result = results.tile([P, GROUP_TILES, HEAD], F32, tag="result")
-            if table is None:
-                nc.vector.tensor_tensor(
-                    out=result[:],
-                    in0=bank[:],
-                    in1=mask_sb[:, tiles].unsqueeze(2).to_broadcast([P, GROUP_TILES, HEAD]),
-                    op=MULT,
-                )
-            else:
-                partner = halves.tile([P, GROUP_TILES, HEAD], F32, tag="partner")
-                nc.vector.tensor_tensor(out=result[:], in0=bank[:], in1=table[:, 0, tiles, :], op=MULT)
-                nc.vector.tensor_tensor(
-                    out=partner[:, :, 0:HALF],
-                    in0=bank[:, :, HALF:HEAD],
-                    in1=table[:, 1, tiles, 0:HALF],
-                    op=MULT,
-                )
-                nc.vector.tensor_tensor(
-                    out=partner[:, :, HALF:HEAD],
-                    in0=bank[:, :, 0:HALF],
-                    in1=table[:, 1, tiles, HALF:HEAD],
-                    op=MULT,
-                )
-                nc.gpsimd.tensor_tensor(out=result[:], in0=result[:], in1=partner[:], op=ADD)
+            partner = halves.tile([P, GROUP_TILES, HEAD], F32, tag="partner")
+            nc.vector.tensor_tensor(out=result[:], in0=bank[:], in1=table[:, 0, tiles, :], op=MULT)
+            nc.vector.tensor_tensor(
+                out=partner[:, :, 0:HALF],
+                in0=bank[:, :, HALF:HEAD],
+                in1=table[:, 1, tiles, 0:HALF],
+                op=MULT,
+            )
+            nc.vector.tensor_tensor(
+                out=partner[:, :, HALF:HEAD],
+                in0=bank[:, :, 0:HALF],
+                in1=table[:, 1, tiles, HALF:HEAD],
+                op=MULT,
+            )
+            nc.gpsimd.tensor_tensor(out=result[:], in0=result[:], in1=partner[:], op=ADD)
             nc.sync.dma_start(
                 out=dest.rearrange("(p j) d -> p j d", j=TILES)[:, tiles, :], in_=result[:]
             )
@@ -282,3 +293,42 @@ def tile_multiheadattention_pa_kernel(
                 biased_of[i] = project(units[i])
             for i in range(first, min(first + UNITS_PER_ROUND, len(units))):
                 finish(units[i], biased_of[i])
+            this_round = first // UNITS_PER_ROUND
+            if 1 <= this_round <= TILES // 2:
+                mask_bv(2 * this_round - 2)
+                mask_bv(2 * this_round - 1)
+
+        v_cols = slice(HEAD * (Q_HEADS + K_HEADS), HEAD * HEADS)
+        for group in range(GROUPS):
+            v_result = results.tile([P, V_HEADS, GROUP_TILES, HEAD], F32, tag="v_result", bufs=2)
+            for t in range(GROUP_TILES):
+                j = GROUP_TILES * group + t
+                tokens = slice(P * t, P * (t + 1))
+                if j % 2 == 0:
+                    v_acc = sums.tile([P, V_HEADS, HEAD], F32, tag="acc")
+                else:
+                    v_acc = banks.tile([P, V_HEADS, HEAD], F32, tag="bank")
+                for g in range(PASSES):
+                    nc.tensor.matmul_mx(
+                        out=v_acc[:].rearrange("p h d -> p (h d)"),
+                        lhsT=x_codes[:, group, g, tokens].bitcast(FP8X4),
+                        lhsT_scale=x_planes[:, group, g, tokens],
+                        rhs=w_words[:, g, v_cols].bitcast(FP8X4),
+                        rhs_scale=w_planes[4 * g : P, v_cols],
+                        start=(g == 0),
+                        stop=(g == PASSES - 1),
+                    )
+                nc.vector.scalar_tensor_tensor(
+                    out=v_result[:, :, t, :],
+                    in0=v_acc[:],
+                    scalar=mask_f32[:, j : j + 1],
+                    in1=bv_masked[:, j, :].rearrange("p (h d) -> p h d", h=V_HEADS),
+                    op0=MULT,
+                    op1=ADD,
+                )
+            tiles = slice(GROUP_TILES * group, GROUP_TILES * (group + 1))
+            for h in range(V_HEADS):
+                nc.sync.dma_start(
+                    out=out_2[0, h].rearrange("(p j) d -> p j d", j=TILES)[:, tiles, :],
+                    in_=v_result[:, h, :, :],
+                )

@@ -138,11 +138,12 @@ def tile_multiheadattention_pa_kernel(
         for j in range(TILES):
             load_x(j)
         load_scales(Wq_scales, 0, Q_HEADS)
-        load_scales(Wk_scales, Q_HEADS, K_HEADS)
-        load_scales(Wv_scales, Q_HEADS + K_HEADS, V_HEADS)
-        load_words(Wq_words, 0, 0, Q_CHUNK)
+        load_words(Wq_words, 0, 0, HEAD)
+        load_words(Wq_words, 0, HEAD, Q_CHUNK)
         load_table(raw_cos, cos)
         load_table(raw_sin, sin)
+        load_scales(Wk_scales, Q_HEADS, K_HEADS)
+        load_scales(Wv_scales, Q_HEADS + K_HEADS, V_HEADS)
         for lo in range(Q_CHUNK, Q_HEADS * HEAD, Q_CHUNK):
             load_words(Wq_words, 0, lo, lo + Q_CHUNK)
         load_words(Wk_words, Q_HEADS, 0, K_HEADS * HEAD)
@@ -197,17 +198,18 @@ def tile_multiheadattention_pa_kernel(
         nc.tensor.transpose(out=bias_bank[:, 0, :], in_=bias_rows_f32[:], identity=ident[:])
         nc.vector.tensor_copy(out=bias_cols[:], in_=bias_bank[:, 0, :])
         nc.vector.tensor_copy(out=mask_f32[:], in_=mask_sb[:])
-        bv_bank = banks.tile([P, GROUP_TILES, P], F32, tag="bank")
-        for h in range(V_HEADS):
-            column = Q_HEADS + K_HEADS + h
-            nc.tensor.transpose(
-                out=bv_bank[:, h, :],
-                in_=bias_cols[:, column : column + 1].to_broadcast([P, P]),
-                identity=ident[:],
+        def spread_bv():
+            bv_bank = banks.tile([P, GROUP_TILES, P], F32, tag="bank")
+            for h in range(V_HEADS):
+                column = Q_HEADS + K_HEADS + h
+                nc.tensor.transpose(
+                    out=bv_bank[:, h, :],
+                    in_=bias_cols[:, column : column + 1].to_broadcast([P, P]),
+                    identity=ident[:],
+                )
+            nc.vector.tensor_copy(
+                out=bv_rows[:], in_=bv_bank[:, 0:V_HEADS, :].rearrange("p h d -> p (h d)")
             )
-        nc.vector.tensor_copy(
-            out=bv_rows[:], in_=bv_bank[:, 0:V_HEADS, :].rearrange("p h d -> p (h d)")
-        )
 
         def mask_bv(j):
             nc.scalar.activation(
@@ -294,6 +296,8 @@ def tile_multiheadattention_pa_kernel(
             for i in range(first, min(first + UNITS_PER_ROUND, len(units))):
                 finish(units[i], biased_of[i])
             this_round = first // UNITS_PER_ROUND
+            if this_round == 0:
+                spread_bv()
             if 1 <= this_round <= TILES // 2:
                 mask_bv(2 * this_round - 2)
                 mask_bv(2 * this_round - 1)

@@ -168,10 +168,7 @@ def tile_multiheadattention_pa_kernel(
                 .rearrange("p (a s u) -> p a s u", a=2, u=2)
             )
             bank_words = bank[:].rearrange("p (a u) s -> p a s u", u=2)
-            if (2 * j + pair) % 4 == 3:
-                nc.vector.tensor_copy(out=grouped_words, in_=bank_words)
-            else:
-                nc.scalar.copy(out=grouped_words, in_=bank_words)
+            nc.scalar.copy(out=grouped_words, in_=bank_words)
             return grouped
 
         def quantise_x(j, pair, grouped):
@@ -184,7 +181,8 @@ def tile_multiheadattention_pa_kernel(
                     in_=grouped[:, a].rearrange("p s t -> p (s t)"),
                 )
 
-        nc.vector.tensor_copy(out=bias_rows_f32[:], in_=bias_rows[:])
+        nc.gpsimd.tensor_copy(out=bias_rows_f32[:], in_=bias_rows[:])
+        nc.gpsimd.tensor_copy(out=mask_f32[:], in_=mask_sb[:])
         waiting = None
         for j in range(TILES):
             for pair in range(PASSES // 2):
@@ -196,8 +194,7 @@ def tile_multiheadattention_pa_kernel(
 
         bias_bank = banks.tile([P, GROUP_TILES, P], F32, tag="bank")
         nc.tensor.transpose(out=bias_bank[:, 0, :], in_=bias_rows_f32[:], identity=ident[:])
-        nc.vector.tensor_copy(out=bias_cols[:], in_=bias_bank[:, 0, :])
-        nc.vector.tensor_copy(out=mask_f32[:], in_=mask_sb[:])
+        nc.scalar.copy(out=bias_cols[:], in_=bias_bank[:, 0, :])
         def spread_bv():
             bv_bank = banks.tile([P, GROUP_TILES, P], F32, tag="bank")
             for h in range(V_HEADS):
@@ -273,15 +270,9 @@ def tile_multiheadattention_pa_kernel(
             partner = halves.tile([P, GROUP_TILES, HEAD], F32, tag="partner")
             nc.vector.tensor_tensor(out=result[:], in0=bank[:], in1=table[:, 0, tiles, :], op=MULT)
             nc.vector.tensor_tensor(
-                out=partner[:, :, 0:HALF],
-                in0=bank[:, :, HALF:HEAD],
-                in1=table[:, 1, tiles, 0:HALF],
-                op=MULT,
-            )
-            nc.vector.tensor_tensor(
-                out=partner[:, :, HALF:HEAD],
-                in0=bank[:, :, 0:HALF],
-                in1=table[:, 1, tiles, HALF:HEAD],
+                out=partner[:].rearrange("p t (h d) -> p t h d", h=2),
+                in0=bank[:].rearrange("p t (h d) -> p t h d", h=2)[:, :, ::-1, :],
+                in1=table[:, 1, tiles, :].rearrange("p t (h d) -> p t h d", h=2),
                 op=MULT,
             )
             nc.gpsimd.tensor_tensor(out=result[:], in0=result[:], in1=partner[:], op=ADD)
@@ -303,6 +294,16 @@ def tile_multiheadattention_pa_kernel(
                 mask_bv(2 * this_round - 1)
 
         v_cols = slice(HEAD * (Q_HEADS + K_HEADS), HEAD * HEADS)
+
+        def store_v(v_result, group, lo, hi):
+            for h in range(V_HEADS):
+                nc.sync.dma_start(
+                    out=out_2[0, h].rearrange("(p j) d -> p j d", j=TILES)[
+                        :, GROUP_TILES * group + lo : GROUP_TILES * group + hi, :
+                    ],
+                    in_=v_result[:, h, lo:hi, :],
+                )
+
         for group in range(GROUPS):
             v_result = results.tile([P, V_HEADS, GROUP_TILES, HEAD], F32, tag="v_result", bufs=2)
             for t in range(GROUP_TILES):
@@ -330,9 +331,9 @@ def tile_multiheadattention_pa_kernel(
                     op0=MULT,
                     op1=ADD,
                 )
-            tiles = slice(GROUP_TILES * group, GROUP_TILES * (group + 1))
-            for h in range(V_HEADS):
-                nc.sync.dma_start(
-                    out=out_2[0, h].rearrange("(p j) d -> p j d", j=TILES)[:, tiles, :],
-                    in_=v_result[:, h, :, :],
-                )
+                if group == GROUPS - 1 and t == GROUP_TILES - 2:
+                    store_v(v_result, group, 0, GROUP_TILES - 1)
+            if group == GROUPS - 1:
+                store_v(v_result, group, GROUP_TILES - 1, GROUP_TILES)
+            else:
+                store_v(v_result, group, 0, GROUP_TILES)

@@ -34,7 +34,7 @@ GROUP_TOKENS = GROUP_TILES * P
 GROUPS = TILES // GROUP_TILES
 Q_CHUNK = 256
 
-UNITS_PER_ROUND = 3
+UNITS_PER_ROUND = 2
 
 FLOPS = 2 * TOKENS * HIDDEN * HEADS * HEAD
 BYTES = (

@@ -35,6 +35,8 @@ GROUPS = TILES // GROUP_TILES
 Q_CHUNK = 256
 
 UNITS_PER_ROUND = 2
+WARM_UP = 5
+WARM_PER_TILE = 2
 
 FLOPS = 2 * TOKENS * HIDDEN * HEADS * HEAD
 BYTES = (
@@ -96,6 +98,8 @@ def tile_multiheadattention_pa_kernel(
         rope_q = keep.tile([P, 2, TILES, HEAD], F32)
         rope_k = keep.tile([P, 2, TILES, HEAD], F32)
 
+        idle_work = keep.tile([P, GROUP_TOKENS], BF16)
+        nc.vector.memset(idle_work[:], 0.0)
         make_identity(nc, ident[:])
         nc.vector.memset(w_planes[:].bitcast(I32), 0)
         nc.vector.memset(bias_rows[:], 0.0)
@@ -181,6 +185,14 @@ def tile_multiheadattention_pa_kernel(
                     in_=grouped[:, a].rearrange("p s t -> p (s t)"),
                 )
 
+        def keep_warm(count):
+            unread = sums.tile([P, GROUP_TOKENS], F32, tag="acc")
+            for i in range(count):
+                nc.tensor.matmul(
+                    out=unread[:], lhsT=idle_work[:, 0:P], rhs=idle_work[:], start=True, stop=True
+                )
+
+        keep_warm(WARM_UP)
         nc.gpsimd.tensor_copy(out=bias_rows_f32[:], in_=bias_rows[:])
         nc.gpsimd.tensor_copy(out=mask_f32[:], in_=mask_sb[:])
         waiting = None
@@ -190,6 +202,7 @@ def tile_multiheadattention_pa_kernel(
                 if waiting is not None:
                     quantise_x(*waiting)
                 waiting = (j, pair, grouped)
+            keep_warm(WARM_PER_TILE)
         quantise_x(*waiting)
 
         bias_bank = banks.tile([P, GROUP_TILES, P], F32, tag="bank")

@@ -37,6 +37,7 @@ Q_CHUNK = 256
 UNITS_PER_ROUND = 2
 WARM_UP = 5
 WARM_PER_TILE = 2
+V_LAG = 2
 
 FLOPS = 2 * TOKENS * HIDDEN * HEADS * HEAD
 BYTES = (
@@ -139,7 +140,11 @@ def tile_multiheadattention_pa_kernel(
                 in_=table[:, 0].rearrange("c (p j) d -> p c (j d)", j=TILES),
             )
 
-        for j in range(TILES):
+        for j in range(V_LAG + 1):
+            load_x(j)
+        load_scales(Wv_scales, Q_HEADS + K_HEADS, V_HEADS)
+        load_words(Wv_words, Q_HEADS + K_HEADS, 0, V_HEADS * HEAD)
+        for j in range(V_LAG + 1, TILES):
             load_x(j)
         load_scales(Wq_scales, 0, Q_HEADS)
         load_words(Wq_words, 0, 0, HEAD)
@@ -147,11 +152,9 @@ def tile_multiheadattention_pa_kernel(
         load_table(raw_cos, cos)
         load_table(raw_sin, sin)
         load_scales(Wk_scales, Q_HEADS, K_HEADS)
-        load_scales(Wv_scales, Q_HEADS + K_HEADS, V_HEADS)
         for lo in range(Q_CHUNK, Q_HEADS * HEAD, Q_CHUNK):
             load_words(Wq_words, 0, lo, lo + Q_CHUNK)
         load_words(Wk_words, Q_HEADS, 0, K_HEADS * HEAD)
-        load_words(Wv_words, Q_HEADS + K_HEADS, 0, V_HEADS * HEAD)
 
         def turn_x(j, pair):
             bank = banks.tile([P, GROUP_TILES, P], F32, tag="bank")
@@ -195,19 +198,11 @@ def tile_multiheadattention_pa_kernel(
         keep_warm(WARM_UP)
         nc.gpsimd.tensor_copy(out=bias_rows_f32[:], in_=bias_rows[:])
         nc.gpsimd.tensor_copy(out=mask_f32[:], in_=mask_sb[:])
-        waiting = None
-        for j in range(TILES):
-            for pair in range(PASSES // 2):
-                grouped = turn_x(j, pair)
-                if waiting is not None:
-                    quantise_x(*waiting)
-                waiting = (j, pair, grouped)
-            keep_warm(WARM_PER_TILE)
-        quantise_x(*waiting)
+        def turn_biases():
+            bias_bank = banks.tile([P, GROUP_TILES, P], F32, tag="bank")
+            nc.tensor.transpose(out=bias_bank[:, 0, :], in_=bias_rows_f32[:], identity=ident[:])
+            nc.scalar.copy(out=bias_cols[:], in_=bias_bank[:, 0, :])
 
-        bias_bank = banks.tile([P, GROUP_TILES, P], F32, tag="bank")
-        nc.tensor.transpose(out=bias_bank[:, 0, :], in_=bias_rows_f32[:], identity=ident[:])
-        nc.scalar.copy(out=bias_cols[:], in_=bias_bank[:, 0, :])
         def spread_bv():
             bv_bank = banks.tile([P, GROUP_TILES, P], F32, tag="bank")
             for h in range(V_HEADS):
@@ -225,6 +220,66 @@ def tile_multiheadattention_pa_kernel(
             nc.scalar.activation(
                 out=bv_masked[:, j, :], in_=bv_rows[:], func=COPY, scale=mask_f32[:, j : j + 1]
             )
+
+        v_cols = slice(HEAD * (Q_HEADS + K_HEADS), HEAD * HEADS)
+        v_results = []
+        for group in range(GROUPS):
+            v_result = results.tile([P, V_HEADS, GROUP_TILES, HEAD], F32, tag="v_result", bufs=GROUPS)
+            v_results.append(v_result)
+
+        def store_v(group, lo, hi):
+            for h in range(V_HEADS):
+                nc.sync.dma_start(
+                    out=out_2[0, h].rearrange("(p j) d -> p j d", j=TILES)[
+                        :, GROUP_TILES * group + lo : GROUP_TILES * group + hi, :
+                    ],
+                    in_=v_results[group][:, h, lo:hi, :],
+                )
+
+        def project_v(j):
+            group, t = divmod(j, GROUP_TILES)
+            tokens = slice(P * t, P * (t + 1))
+            v_acc = sums.tile([P, V_HEADS, HEAD], F32, tag="acc")
+            for g in range(PASSES):
+                nc.tensor.matmul_mx(
+                    out=v_acc[:].rearrange("p h d -> p (h d)"),
+                    lhsT=x_codes[:, group, g, tokens].bitcast(FP8X4),
+                    lhsT_scale=x_planes[:, group, g, tokens],
+                    rhs=w_words[:, g, v_cols].bitcast(FP8X4),
+                    rhs_scale=w_planes[4 * g : P, v_cols],
+                    start=(g == 0),
+                    stop=(g == PASSES - 1),
+                )
+            nc.vector.scalar_tensor_tensor(
+                out=v_results[group][:, :, t, :],
+                in0=v_acc[:],
+                scalar=mask_f32[:, j : j + 1],
+                in1=bv_masked[:, j, :].rearrange("p (h d) -> p h d", h=V_HEADS),
+                op0=MULT,
+                op1=ADD,
+            )
+
+        waiting = None
+        for j in range(TILES):
+            for pair in range(PASSES // 2):
+                grouped = turn_x(j, pair)
+                if waiting is not None:
+                    quantise_x(*waiting)
+                waiting = (j, pair, grouped)
+            if j == 0:
+                turn_biases()
+            if j == 1:
+                spread_bv()
+            if j < V_LAG:
+                keep_warm(WARM_PER_TILE)
+            else:
+                mask_bv(j - V_LAG)
+                project_v(j - V_LAG)
+                if j - V_LAG == GROUP_TILES - 1:
+                    store_v(0, 0, GROUP_TILES)
+        quantise_x(*waiting)
+        for j in range(TILES - V_LAG, TILES):
+            mask_bv(j)
 
         lo = 0
         for i in range(2 * len(SECTIONS)):
@@ -299,54 +354,9 @@ def tile_multiheadattention_pa_kernel(
                 biased_of[i] = project(units[i])
             for i in range(first, min(first + UNITS_PER_ROUND, len(units))):
                 finish(units[i], biased_of[i])
-            this_round = first // UNITS_PER_ROUND
-            if this_round == 0:
-                spread_bv()
-            if 1 <= this_round <= TILES // 2:
-                mask_bv(2 * this_round - 2)
-                mask_bv(2 * this_round - 1)
 
-        v_cols = slice(HEAD * (Q_HEADS + K_HEADS), HEAD * HEADS)
-
-        def store_v(v_result, group, lo, hi):
-            for h in range(V_HEADS):
-                nc.sync.dma_start(
-                    out=out_2[0, h].rearrange("(p j) d -> p j d", j=TILES)[
-                        :, GROUP_TILES * group + lo : GROUP_TILES * group + hi, :
-                    ],
-                    in_=v_result[:, h, lo:hi, :],
-                )
-
-        for group in range(GROUPS):
-            v_result = results.tile([P, V_HEADS, GROUP_TILES, HEAD], F32, tag="v_result", bufs=2)
-            for t in range(GROUP_TILES):
-                j = GROUP_TILES * group + t
-                tokens = slice(P * t, P * (t + 1))
-                if j % 2 == 0:
-                    v_acc = sums.tile([P, V_HEADS, HEAD], F32, tag="acc")
-                else:
-                    v_acc = banks.tile([P, V_HEADS, HEAD], F32, tag="bank")
-                for g in range(PASSES):
-                    nc.tensor.matmul_mx(
-                        out=v_acc[:].rearrange("p h d -> p (h d)"),
-                        lhsT=x_codes[:, group, g, tokens].bitcast(FP8X4),
-                        lhsT_scale=x_planes[:, group, g, tokens],
-                        rhs=w_words[:, g, v_cols].bitcast(FP8X4),
-                        rhs_scale=w_planes[4 * g : P, v_cols],
-                        start=(g == 0),
-                        stop=(g == PASSES - 1),
-                    )
-                nc.vector.scalar_tensor_tensor(
-                    out=v_result[:, :, t, :],
-                    in0=v_acc[:],
-                    scalar=mask_f32[:, j : j + 1],
-                    in1=bv_masked[:, j, :].rearrange("p (h d) -> p h d", h=V_HEADS),
-                    op0=MULT,
-                    op1=ADD,
-                )
-                if group == GROUPS - 1 and t == GROUP_TILES - 2:
-                    store_v(v_result, group, 0, GROUP_TILES - 1)
-            if group == GROUPS - 1:
-                store_v(v_result, group, GROUP_TILES - 1, GROUP_TILES)
-            else:
-                store_v(v_result, group, 0, GROUP_TILES)
+        for j in range(TILES - V_LAG, TILES):
+            project_v(j)
+            if j == TILES - 2:
+                store_v(GROUPS - 1, 0, GROUP_TILES - 1)
+        store_v(GROUPS - 1, GROUP_TILES - 1, GROUP_TILES)

@@ -38,6 +38,8 @@ UNITS_PER_ROUND = 2
 WARM_UP = 5
 WARM_PER_TILE = 2
 V_LAG = 2
+HEAD_UNITS = 3
+HEAD_V_TILES = TILES - V_LAG - HEAD_UNITS
 
 FLOPS = 2 * TOKENS * HIDDEN * HEADS * HEAD
 BYTES = (
@@ -144,15 +146,18 @@ def tile_multiheadattention_pa_kernel(
             load_x(j)
         load_scales(Wv_scales, Q_HEADS + K_HEADS, V_HEADS)
         load_words(Wv_words, Q_HEADS + K_HEADS, 0, V_HEADS * HEAD)
-        for j in range(V_LAG + 1, TILES):
+        for j in range(V_LAG + 1, TILES - HEAD_UNITS + 1):
             load_x(j)
         load_scales(Wq_scales, 0, Q_HEADS)
-        load_words(Wq_words, 0, 0, HEAD)
-        load_words(Wq_words, 0, HEAD, Q_CHUNK)
+        for h in range(HEAD_UNITS):
+            load_words(Wq_words, 0, HEAD * h, HEAD * (h + 1))
+            if TILES - HEAD_UNITS + 1 + h < TILES:
+                load_x(TILES - HEAD_UNITS + 1 + h)
         load_table(raw_cos, cos)
         load_table(raw_sin, sin)
+        load_words(Wq_words, 0, HEAD * HEAD_UNITS, HEAD * (HEAD_UNITS + 1))
         load_scales(Wk_scales, Q_HEADS, K_HEADS)
-        for lo in range(Q_CHUNK, Q_HEADS * HEAD, Q_CHUNK):
+        for lo in range(HEAD * (HEAD_UNITS + 1), Q_HEADS * HEAD, Q_CHUNK):
             load_words(Wq_words, 0, lo, lo + Q_CHUNK)
         load_words(Wk_words, Q_HEADS, 0, K_HEADS * HEAD)
 
@@ -239,7 +244,10 @@ def tile_multiheadattention_pa_kernel(
         def project_v(j):
             group, t = divmod(j, GROUP_TILES)
             tokens = slice(P * t, P * (t + 1))
-            v_acc = sums.tile([P, V_HEADS, HEAD], F32, tag="acc")
+            if j % 2 == 0:
+                v_acc = sums.tile([P, V_HEADS, HEAD], F32, tag="acc")
+            else:
+                v_acc = banks.tile([P, V_HEADS, HEAD], F32, tag="bank")
             for g in range(PASSES):
                 nc.tensor.matmul_mx(
                     out=v_acc[:].rearrange("p h d -> p (h d)"),
@@ -250,6 +258,10 @@ def tile_multiheadattention_pa_kernel(
                     start=(g == 0),
                     stop=(g == PASSES - 1),
                 )
+            return v_acc
+
+        def finish_v(j, v_acc):
+            group, t = divmod(j, GROUP_TILES)
             nc.vector.scalar_tensor_tensor(
                 out=v_results[group][:, :, t, :],
                 in0=v_acc[:],
@@ -259,52 +271,13 @@ def tile_multiheadattention_pa_kernel(
                 op1=ADD,
             )
 
-        waiting = None
-        for j in range(TILES):
-            for pair in range(PASSES // 2):
-                grouped = turn_x(j, pair)
-                if waiting is not None:
-                    quantise_x(*waiting)
-                waiting = (j, pair, grouped)
-            if j == 0:
-                turn_biases()
-            if j == 1:
-                spread_bv()
-            if j < V_LAG:
-                keep_warm(WARM_PER_TILE)
-            else:
-                mask_bv(j - V_LAG)
-                project_v(j - V_LAG)
-                if j - V_LAG == GROUP_TILES - 1:
-                    store_v(0, 0, GROUP_TILES)
-        quantise_x(*waiting)
-        for j in range(TILES - V_LAG, TILES):
-            mask_bv(j)
-
-        lo = 0
-        for i in range(2 * len(SECTIONS)):
-            c = i % len(SECTIONS)
-            hi = lo + SECTIONS[c]
-            nc.vector.tensor_copy(out=rope_q[:, 0, :, lo:hi], in_=raw_cos[:, c, :, lo:hi])
-            nc.gpsimd.tensor_scalar(
-                out=rope_q[:, 1, :, lo:hi],
-                in0=raw_sin[:, c, :, lo:hi],
-                scalar1=(-1.0 if lo < HALF else 1.0),
-                scalar2=0.0,
-                op0=MULT,
-                op1=ADD,
-            )
-            lo = hi
-        mask_of_row = mask_sb[:].unsqueeze(2).to_broadcast([P, TILES, HEAD])
-        nc.vector.tensor_tensor(out=rope_k[:, 0], in0=rope_q[:, 0], in1=mask_of_row, op=MULT)
-        nc.gpsimd.tensor_tensor(out=rope_k[:, 1], in0=rope_q[:, 1], in1=mask_of_row, op=MULT)
-
         heads = []
         for h in range(Q_HEADS):
             heads.append((h, rope_q, out_0[0, h]))
         for h in range(K_HEADS):
             heads.append((Q_HEADS + h, rope_k, out_1[0, h]))
-        units = [(head, group) for head in heads for group in range(GROUPS)]
+        units = [(head, group) for group in range(GROUPS) for head in heads[0:HEAD_UNITS]]
+        units.extend([(head, group) for head in heads[HEAD_UNITS:] for group in range(GROUPS)])
 
         def project(unit):
             (head, table, dest), group = unit
@@ -326,13 +299,16 @@ def tile_multiheadattention_pa_kernel(
             )
             return biased
 
-        def finish(unit, biased):
-            (head, table, dest), group = unit
+        def turn_back(biased):
             bank = banks.tile([P, GROUP_TILES, HEAD], F32, tag="bank")
             for t in range(GROUP_TILES):
                 nc.tensor.transpose(
                     out=bank[:, t, :], in_=biased[:, P * t : P * (t + 1)], identity=ident[:]
                 )
+            return bank
+
+        def rotate(unit, bank):
+            (head, table, dest), group = unit
             tiles = slice(GROUP_TILES * group, GROUP_TILES * (group + 1))
             result = results.tile([P, GROUP_TILES, HEAD], F32, tag="result")
             partner = halves.tile([P, GROUP_TILES, HEAD], F32, tag="partner")
@@ -348,15 +324,72 @@ def tile_multiheadattention_pa_kernel(
                 out=dest.rearrange("(p j) d -> p j d", j=TILES)[:, tiles, :], in_=result[:]
             )
 
-        biased_of = {0: project(units[0])}
-        for first in range(0, len(units), UNITS_PER_ROUND):
-            for i in range(first + 1, min(first + 1 + UNITS_PER_ROUND, len(units))):
+        biased_of = {}
+        waiting = None
+        for j in range(TILES):
+            for pair in range(PASSES // 2):
+                grouped = turn_x(j, pair)
+                if waiting is not None:
+                    quantise_x(*waiting)
+                waiting = (j, pair, grouped)
+            if j == 0:
+                turn_biases()
+            if j == 1:
+                spread_bv()
+            if j < V_LAG:
+                keep_warm(WARM_PER_TILE)
+            elif j < V_LAG + HEAD_V_TILES:
+                mask_bv(j - V_LAG)
+                finish_v(j - V_LAG, project_v(j - V_LAG))
+            else:
+                i = j - V_LAG - HEAD_V_TILES
                 biased_of[i] = project(units[i])
-            for i in range(first, min(first + UNITS_PER_ROUND, len(units))):
-                finish(units[i], biased_of[i])
+        quantise_x(*waiting)
+        for j in range(HEAD_V_TILES, TILES):
+            mask_bv(j)
 
-        for j in range(TILES - V_LAG, TILES):
-            project_v(j)
+        lo = 0
+        for i in range(2 * len(SECTIONS)):
+            c = i % len(SECTIONS)
+            hi = lo + SECTIONS[c]
+            nc.vector.tensor_copy(out=rope_q[:, 0, :, lo:hi], in_=raw_cos[:, c, :, lo:hi])
+            nc.gpsimd.tensor_scalar(
+                out=rope_q[:, 1, :, lo:hi],
+                in0=raw_sin[:, c, :, lo:hi],
+                scalar1=(-1.0 if lo < HALF else 1.0),
+                scalar2=0.0,
+                op0=MULT,
+                op1=ADD,
+            )
+            lo = hi
+
+        def mask_tables(j):
+            nc.scalar.activation(
+                out=rope_k[:, :, j, :], in_=rope_q[:, :, j, :], func=COPY, scale=mask_f32[:, j : j + 1]
+            )
+
+        for first in range(0, len(units) - UNITS_PER_ROUND, UNITS_PER_ROUND):
+            for i in range(first, first + UNITS_PER_ROUND):
+                rotate(units[i], turn_back(biased_of[i]))
+            for i in range(first + HEAD_UNITS, min(first + HEAD_UNITS + UNITS_PER_ROUND, len(units))):
+                biased_of[i] = project(units[i])
+            this_round = first // UNITS_PER_ROUND
+            if 1 <= this_round <= TILES // 2:
+                mask_tables(2 * this_round - 2)
+                mask_tables(2 * this_round - 1)
+
+        last = [len(units) - 2, len(units) - 1]
+        last_banks = [turn_back(biased_of[i]) for i in last]
+        v_accs = {}
+        v_accs[HEAD_V_TILES] = project_v(HEAD_V_TILES)
+        rotate(units[last[0]], last_banks[0])
+        finish_v(HEAD_V_TILES, v_accs[HEAD_V_TILES])
+        store_v(0, 0, GROUP_TILES)
+        v_accs[HEAD_V_TILES + 1] = project_v(HEAD_V_TILES + 1)
+        rotate(units[last[1]], last_banks[1])
+        finish_v(HEAD_V_TILES + 1, v_accs[HEAD_V_TILES + 1])
+        for j in range(HEAD_V_TILES + 2, TILES):
+            finish_v(j, project_v(j))
             if j == TILES - 2:
                 store_v(GROUPS - 1, 0, GROUP_TILES - 1)
         store_v(GROUPS - 1, GROUP_TILES - 1, GROUP_TILES)

@@ -37,7 +37,7 @@ Q_CHUNK = 256
 UNITS_PER_ROUND = 2
 WARM_UP = 5
 WARM_PER_TILE = 2
-V_LAG = 2
+V_LAG = 1
 HEAD_UNITS = 3
 HEAD_V_TILES = TILES - V_LAG - HEAD_UNITS
 
@@ -217,6 +217,9 @@ def tile_multiheadattention_pa_kernel(
                     in_=bias_cols[:, column : column + 1].to_broadcast([P, P]),
                     identity=ident[:],
                 )
+            return bv_bank
+
+        def keep_bv(bv_bank):
             nc.vector.tensor_copy(
                 out=bv_rows[:], in_=bv_bank[:, 0:V_HEADS, :].rearrange("p h d -> p (h d)")
             )
@@ -270,6 +273,12 @@ def tile_multiheadattention_pa_kernel(
                 op0=MULT,
                 op1=ADD,
             )
+            if j == GROUP_TILES - 1:
+                store_v(0, 0, GROUP_TILES)
+            if j == TILES - 2:
+                store_v(GROUPS - 1, 0, GROUP_TILES - 1)
+            if j == TILES - 1:
+                store_v(GROUPS - 1, GROUP_TILES - 1, GROUP_TILES)
 
         heads = []
         for h in range(Q_HEADS):
@@ -328,14 +337,16 @@ def tile_multiheadattention_pa_kernel(
         waiting = None
         for j in range(TILES):
             for pair in range(PASSES // 2):
+                if (j, pair) == (1, 0):
+                    bv_bank = spread_bv()
                 grouped = turn_x(j, pair)
                 if waiting is not None:
                     quantise_x(*waiting)
                 waiting = (j, pair, grouped)
-            if j == 0:
-                turn_biases()
-            if j == 1:
-                spread_bv()
+                if (j, pair) == (0, 0):
+                    turn_biases()
+                if (j, pair) == (1, 0):
+                    keep_bv(bv_bank)
             if j < V_LAG:
                 keep_warm(WARM_PER_TILE)
             elif j < V_LAG + HEAD_V_TILES:
@@ -380,16 +391,11 @@ def tile_multiheadattention_pa_kernel(
 
         last = [len(units) - 2, len(units) - 1]
         last_banks = [turn_back(biased_of[i]) for i in last]
-        v_accs = {}
-        v_accs[HEAD_V_TILES] = project_v(HEAD_V_TILES)
+        first_acc = project_v(HEAD_V_TILES)
         rotate(units[last[0]], last_banks[0])
-        finish_v(HEAD_V_TILES, v_accs[HEAD_V_TILES])
-        store_v(0, 0, GROUP_TILES)
-        v_accs[HEAD_V_TILES + 1] = project_v(HEAD_V_TILES + 1)
+        finish_v(HEAD_V_TILES, first_acc)
+        second_acc = project_v(HEAD_V_TILES + 1)
         rotate(units[last[1]], last_banks[1])
-        finish_v(HEAD_V_TILES + 1, v_accs[HEAD_V_TILES + 1])
+        finish_v(HEAD_V_TILES + 1, second_acc)
         for j in range(HEAD_V_TILES + 2, TILES):
             finish_v(j, project_v(j))
-            if j == TILES - 2:
-                store_v(GROUPS - 1, 0, GROUP_TILES - 1)
-        store_v(GROUPS - 1, GROUP_TILES - 1, GROUP_TILES)

@@ -35,8 +35,6 @@ GROUPS = TILES // GROUP_TILES
 Q_CHUNK = 256
 
 UNITS_PER_ROUND = 2
-WARM_UP = 5
-WARM_PER_TILE = 2
 V_LAG = 1
 HEAD_UNITS = 3
 HEAD_V_TILES = TILES - V_LAG - HEAD_UNITS
@@ -101,8 +99,6 @@ def tile_multiheadattention_pa_kernel(
         rope_q = keep.tile([P, 2, TILES, HEAD], F32)
         rope_k = keep.tile([P, 2, TILES, HEAD], F32)
 
-        idle_work = keep.tile([P, GROUP_TOKENS], BF16)
-        nc.vector.memset(idle_work[:], 0.0)
         make_identity(nc, ident[:])
         nc.vector.memset(w_planes[:].bitcast(I32), 0)
         nc.vector.memset(bias_rows[:], 0.0)
@@ -193,14 +189,6 @@ def tile_multiheadattention_pa_kernel(
                     in_=grouped[:, a].rearrange("p s t -> p (s t)"),
                 )
 
-        def keep_warm(count):
-            unread = sums.tile([P, GROUP_TOKENS], F32, tag="acc")
-            for i in range(count):
-                nc.tensor.matmul(
-                    out=unread[:], lhsT=idle_work[:, 0:P], rhs=idle_work[:], start=True, stop=True
-                )
-
-        keep_warm(WARM_UP)
         nc.gpsimd.tensor_copy(out=bias_rows_f32[:], in_=bias_rows[:])
         nc.gpsimd.tensor_copy(out=mask_f32[:], in_=mask_sb[:])
         def turn_biases():
@@ -347,12 +335,10 @@ def tile_multiheadattention_pa_kernel(
                     turn_biases()
                 if (j, pair) == (1, 0):
                     keep_bv(bv_bank)
-            if j < V_LAG:
-                keep_warm(WARM_PER_TILE)
-            elif j < V_LAG + HEAD_V_TILES:
+            if V_LAG <= j < V_LAG + HEAD_V_TILES:
                 mask_bv(j - V_LAG)
                 finish_v(j - V_LAG, project_v(j - V_LAG))
-            else:
+            if j >= V_LAG + HEAD_V_TILES:
                 i = j - V_LAG - HEAD_V_TILES
                 biased_of[i] = project(units[i])
         quantise_x(*waiting)

from contextlib import ExitStack

import concourse.mybir as mybir
from concourse.masks import make_identity

F32 = mybir.dt.float32
BF16 = mybir.dt.bfloat16
I32 = mybir.dt.int32
U32 = mybir.dt.uint32
U8 = mybir.dt.uint8
FP8X4 = mybir.dt.float8_e4m3fn_x4
MULT = mybir.AluOpType.mult
ADD = mybir.AluOpType.add
IDENTITY = mybir.ActivationFunctionType.Identity
COPY = mybir.ActivationFunctionType.Copy

P = 128
PACK = 4
TOKENS = 1024
HIDDEN = 2048
HEAD = 128
HALF = HEAD // 2
Q_HEADS = 16
K_HEADS = 2
V_HEADS = 2
HEADS = Q_HEADS + K_HEADS + V_HEADS
SECTIONS = (16, 24, 24)

PASSES = HIDDEN // (P * PACK)
WORDS_PER_PASS = P * PACK // 2
TILES = TOKENS // P
GROUP_TILES = 4
GROUP_TOKENS = GROUP_TILES * P
GROUPS = TILES // GROUP_TILES
Q_CHUNK = 256

UNITS_PER_ROUND = 2
V_LAG = 1
HEAD_UNITS = 3
HEAD_V_TILES = TILES - V_LAG - HEAD_UNITS

FLOPS = 2 * TOKENS * HIDDEN * HEADS * HEAD
BYTES = (
    2 * TOKENS * HIDDEN
    + 2 * 2 * TOKENS * HEAD
    + 2 * TOKENS
    + HIDDEN * HEADS * HEAD
    + HIDDEN // 32 * HEADS * HEAD
    + 2 * HEADS * HEAD
    + 4 * TOKENS * HEADS * HEAD
)


def tile_multiheadattention_pa_kernel(
    tc,
    x,
    cos,
    sin,
    mask,
    Wq_words,
    Wq_scales,
    bq,
    Wk_words,
    Wk_scales,
    bk,
    Wv_words,
    Wv_scales,
    bv,
    out_0,
    out_1,
    out_2,
):
    nc = tc.nc
    with ExitStack() as ctx:
        keep = ctx.enter_context(tc.tile_pool(name="keep", bufs=1))
        stage = ctx.enter_context(tc.tile_pool(name="stage", bufs=4))
        turned = ctx.enter_context(tc.tile_pool(name="turned", bufs=UNITS_PER_ROUND + 2))
        halves = ctx.enter_context(tc.tile_pool(name="halves", bufs=4))
        results = ctx.enter_context(tc.tile_pool(name="results", bufs=12))
        sums = ctx.enter_context(tc.psum_pool(name="sums", bufs=3))
        banks = ctx.enter_context(tc.psum_pool(name="banks", bufs=5))
        ctx.enter_context(tc.manual_schedule())

        ident = keep.tile([P, P], F32)
        x_sb = keep.tile([P, TILES, HIDDEN], BF16)
        w_words = keep.tile([P, PASSES, HEADS * HEAD], U32, align_bytes=64)
        w_planes = keep.tile([P, HEADS * HEAD], U8, align_bytes=64)
        x_codes = keep.tile([P, GROUPS, PASSES, GROUP_TOKENS], U32, align_bytes=64)
        x_planes = keep.tile([P, GROUPS, PASSES, GROUP_TOKENS], U8, align_bytes=64)
        bias_rows = keep.tile([P, HEAD], BF16)
        bias_rows_f32 = keep.tile([P, HEAD], F32)
        bias_cols = keep.tile([P, P], F32)
        mask_sb = keep.tile([P, TILES], BF16)
        mask_f32 = keep.tile([P, TILES], F32)
        bv_masked = keep.tile([P, TILES, V_HEADS * HEAD], F32)
        bv_rows = keep.tile([P, V_HEADS * HEAD], F32)
        raw_cos = keep.tile([P, len(SECTIONS), TILES, HEAD], BF16)
        raw_sin = keep.tile([P, len(SECTIONS), TILES, HEAD], BF16)
        rope_q = keep.tile([P, 2, TILES, HEAD], F32)
        rope_k = keep.tile([P, 2, TILES, HEAD], F32)

        make_identity(nc, ident[:])
        nc.vector.memset(w_planes[:].bitcast(I32), 0)
        nc.vector.memset(bias_rows[:], 0.0)

        nc.scalar.dma_start(out=bias_rows[0:Q_HEADS, :], in_=bq.rearrange("(h d) -> h d", d=HEAD))
        nc.scalar.dma_start(
            out=bias_rows[Q_HEADS : Q_HEADS + K_HEADS, :], in_=bk.rearrange("(h d) -> h d", d=HEAD)
        )
        nc.scalar.dma_start(
            out=bias_rows[Q_HEADS + K_HEADS : HEADS, :], in_=bv.rearrange("(h d) -> h d", d=HEAD)
        )
        nc.scalar.dma_start(out=mask_sb[:], in_=mask[0].rearrange("(p j) -> p j", j=TILES))

        x_rows = x[0].rearrange("(p j) k -> p j k", j=TILES)

        def load_x(j):
            nc.sync.dma_start(out=x_sb[:, j, :], in_=x_rows[:, j, :])

        def load_scales(scales, first_head, heads):
            cols = slice(HEAD * first_head, HEAD * (first_head + heads))
            for quadrant in range(4):
                nc.sync.dma_start(
                    out=w_planes[32 * quadrant : 32 * quadrant + 16, cols].bitcast(I32),
                    in_=scales[:, 4 * quadrant : 4 * quadrant + 4, :].bitcast(I32),
                )

        def load_words(words, first_head, lo, hi):
            first = HEAD * first_head
            nc.sync.dma_start(
                out=w_words[:, :, first + lo : first + hi].bitcast(I32),
                in_=words.rearrange("g p n t -> p g (n t)")[:, :, PACK * lo : PACK * hi].bitcast(I32),
            )

        def load_table(raw, table):
            nc.sync.dma_start(
                out=raw[:].rearrange("p c j d -> p c (j d)"),
                in_=table[:, 0].rearrange("c (p j) d -> p c (j d)", j=TILES),
            )

        for j in range(V_LAG + 1):
            load_x(j)
        load_scales(Wv_scales, Q_HEADS + K_HEADS, V_HEADS)
        load_words(Wv_words, Q_HEADS + K_HEADS, 0, V_HEADS * HEAD)
        for j in range(V_LAG + 1, TILES - HEAD_UNITS + 1):
            load_x(j)
        load_scales(Wq_scales, 0, Q_HEADS)
        for h in range(HEAD_UNITS):
            load_words(Wq_words, 0, HEAD * h, HEAD * (h + 1))
            if TILES - HEAD_UNITS + 1 + h < TILES:
                load_x(TILES - HEAD_UNITS + 1 + h)
        load_table(raw_cos, cos)
        load_table(raw_sin, sin)
        load_words(Wq_words, 0, HEAD * HEAD_UNITS, HEAD * (HEAD_UNITS + 1))
        load_scales(Wk_scales, Q_HEADS, K_HEADS)
        for lo in range(HEAD * (HEAD_UNITS + 1), Q_HEADS * HEAD, Q_CHUNK):
            load_words(Wq_words, 0, lo, lo + Q_CHUNK)
        load_words(Wk_words, Q_HEADS, 0, K_HEADS * HEAD)

        def turn_x(j, pair):
            bank = banks.tile([P, GROUP_TILES, P], F32, tag="bank")
            words = x_sb[:, j, :].bitcast(F32)
            for a in range(2):
                first = WORDS_PER_PASS * (2 * pair + a)
                for u in range(2):
                    nc.tensor.transpose(
                        out=bank[:, 2 * a + u, :],
                        in_=words[:, first + u : first + WORDS_PER_PASS : 2],
                        identity=ident[:],
                    )
            grouped = stage.tile([P, 2, P, PACK], BF16, tag="grouped", align_bytes=64)
            grouped_words = (
                grouped[:]
                .rearrange("p a s t -> p (a s t)")
                .bitcast(F32)
                .rearrange("p (a s u) -> p a s u", a=2, u=2)
            )
            bank_words = bank[:].rearrange("p (a u) s -> p a s u", u=2)
            nc.scalar.copy(out=grouped_words, in_=bank_words)
            return grouped

        def quantise_x(j, pair, grouped):
            group, tile_in_group = divmod(j, GROUP_TILES)
            cols = slice(P * tile_in_group, P * (tile_in_group + 1))
            for a in range(2):
                nc.vector.quantize_mx(
                    out=x_codes[:, group, 2 * pair + a, cols].bitcast(FP8X4),
                    scales=x_planes[:, group, 2 * pair + a, cols],
                    in_=grouped[:, a].rearrange("p s t -> p (s t)"),
                )

        nc.gpsimd.tensor_copy(out=bias_rows_f32[:], in_=bias_rows[:])
        nc.gpsimd.tensor_copy(out=mask_f32[:], in_=mask_sb[:])
        def turn_biases():
            bias_bank = banks.tile([P, GROUP_TILES, P], F32, tag="bank")
            nc.tensor.transpose(out=bias_bank[:, 0, :], in_=bias_rows_f32[:], identity=ident[:])
            nc.scalar.copy(out=bias_cols[:], in_=bias_bank[:, 0, :])

        def spread_bv():
            bv_bank = banks.tile([P, GROUP_TILES, P], F32, tag="bank")
            for h in range(V_HEADS):
                column = Q_HEADS + K_HEADS + h
                nc.tensor.transpose(
                    out=bv_bank[:, h, :],
                    in_=bias_cols[:, column : column + 1].to_broadcast([P, P]),
                    identity=ident[:],
                )
            return bv_bank

        def keep_bv(bv_bank):
            nc.vector.tensor_copy(
                out=bv_rows[:], in_=bv_bank[:, 0:V_HEADS, :].rearrange("p h d -> p (h d)")
            )

        def mask_bv(j):
            nc.scalar.activation(
                out=bv_masked[:, j, :], in_=bv_rows[:], func=COPY, scale=mask_f32[:, j : j + 1]
            )

        v_cols = slice(HEAD * (Q_HEADS + K_HEADS), HEAD * HEADS)
        v_results = []
        for group in range(GROUPS):
            v_result = results.tile([P, V_HEADS, GROUP_TILES, HEAD], F32, tag="v_result", bufs=GROUPS)
            v_results.append(v_result)

        def store_v(group, lo, hi):
            for h in range(V_HEADS):
                nc.sync.dma_start(
                    out=out_2[0, h].rearrange("(p j) d -> p j d", j=TILES)[
                        :, GROUP_TILES * group + lo : GROUP_TILES * group + hi, :
                    ],
                    in_=v_results[group][:, h, lo:hi, :],
                )

        def project_v(j):
            group, t = divmod(j, GROUP_TILES)
            tokens = slice(P * t, P * (t + 1))
            if j % 2 == 0:
                v_acc = sums.tile([P, V_HEADS, HEAD], F32, tag="acc")
            else:
                v_acc = banks.tile([P, V_HEADS, HEAD], F32, tag="bank")
            for g in range(PASSES):
                nc.tensor.matmul_mx(
                    out=v_acc[:].rearrange("p h d -> p (h d)"),
                    lhsT=x_codes[:, group, g, tokens].bitcast(FP8X4),
                    lhsT_scale=x_planes[:, group, g, tokens],
                    rhs=w_words[:, g, v_cols].bitcast(FP8X4),
                    rhs_scale=w_planes[4 * g : P, v_cols],
                    start=(g == 0),
                    stop=(g == PASSES - 1),
                )
            return v_acc

        def finish_v(j, v_acc):
            group, t = divmod(j, GROUP_TILES)
            nc.vector.scalar_tensor_tensor(
                out=v_results[group][:, :, t, :],
                in0=v_acc[:],
                scalar=mask_f32[:, j : j + 1],
                in1=bv_masked[:, j, :].rearrange("p (h d) -> p h d", h=V_HEADS),
                op0=MULT,
                op1=ADD,
            )
            if j == GROUP_TILES - 1:
                store_v(0, 0, GROUP_TILES)
            if j == TILES - 2:
                store_v(GROUPS - 1, 0, GROUP_TILES - 1)
            if j == TILES - 1:
                store_v(GROUPS - 1, GROUP_TILES - 1, GROUP_TILES)

        heads = []
        for h in range(Q_HEADS):
            heads.append((h, rope_q, out_0[0, h]))
        for h in range(K_HEADS):
            heads.append((Q_HEADS + h, rope_k, out_1[0, h]))
        units = [(head, group) for group in range(GROUPS) for head in heads[0:HEAD_UNITS]]
        units.extend([(head, group) for head in heads[HEAD_UNITS:] for group in range(GROUPS)])

        def project(unit):
            (head, table, dest), group = unit
            cols = slice(HEAD * head, HEAD * (head + 1))
            acc = sums.tile([P, GROUP_TOKENS], F32, tag="acc")
            for g in range(PASSES):
                nc.tensor.matmul_mx(
                    out=acc[:],
                    lhsT=w_words[:, g, cols].bitcast(FP8X4),
                    lhsT_scale=w_planes[4 * g : P, cols],
                    rhs=x_codes[:, group, g, :].bitcast(FP8X4),
                    rhs_scale=x_planes[:, group, g, :],
                    start=(g == 0),
                    stop=(g == PASSES - 1),
                )
            biased = turned.tile([P, GROUP_TOKENS], F32, tag="biased")
            nc.scalar.activation(
                out=biased[:], in_=acc[:], func=IDENTITY, bias=bias_cols[:, head : head + 1], scale=1.0
            )
            return biased

        def turn_back(biased):
            bank = banks.tile([P, GROUP_TILES, HEAD], F32, tag="bank")
            for t in range(GROUP_TILES):
                nc.tensor.transpose(
                    out=bank[:, t, :], in_=biased[:, P * t : P * (t + 1)], identity=ident[:]
                )
            return bank

        def rotate(unit, bank):
            (head, table, dest), group = unit
            tiles = slice(GROUP_TILES * group, GROUP_TILES * (group + 1))
            result = results.tile([P, GROUP_TILES, HEAD], F32, tag="result")
            partner = halves.tile([P, GROUP_TILES, HEAD], F32, tag="partner")
            nc.vector.tensor_tensor(out=result[:], in0=bank[:], in1=table[:, 0, tiles, :], op=MULT)
            nc.vector.tensor_tensor(
                out=partner[:].rearrange("p t (h d) -> p t h d", h=2),
                in0=bank[:].rearrange("p t (h d) -> p t h d", h=2)[:, :, ::-1, :],
                in1=table[:, 1, tiles, :].rearrange("p t (h d) -> p t h d", h=2),
                op=MULT,
            )
            nc.gpsimd.tensor_tensor(out=result[:], in0=result[:], in1=partner[:], op=ADD)
            nc.sync.dma_start(
                out=dest.rearrange("(p j) d -> p j d", j=TILES)[:, tiles, :], in_=result[:]
            )

        biased_of = {}
        waiting = None
        for j in range(TILES):
            for pair in range(PASSES // 2):
                if (j, pair) == (1, 0):
                    bv_bank = spread_bv()
                grouped = turn_x(j, pair)
                if waiting is not None:
                    quantise_x(*waiting)
                waiting = (j, pair, grouped)
                if (j, pair) == (0, 0):
                    turn_biases()
                if (j, pair) == (1, 0):
                    keep_bv(bv_bank)
            if V_LAG <= j < V_LAG + HEAD_V_TILES:
                mask_bv(j - V_LAG)
                finish_v(j - V_LAG, project_v(j - V_LAG))
            if j >= V_LAG + HEAD_V_TILES:
                i = j - V_LAG - HEAD_V_TILES
                biased_of[i] = project(units[i])
        quantise_x(*waiting)
        for j in range(HEAD_V_TILES, TILES):
            mask_bv(j)

        lo = 0
        for i in range(2 * len(SECTIONS)):
            c = i % len(SECTIONS)
            hi = lo + SECTIONS[c]
            nc.vector.tensor_copy(out=rope_q[:, 0, :, lo:hi], in_=raw_cos[:, c, :, lo:hi])
            nc.gpsimd.tensor_scalar(
                out=rope_q[:, 1, :, lo:hi],
                in0=raw_sin[:, c, :, lo:hi],
                scalar1=(-1.0 if lo < HALF else 1.0),
                scalar2=0.0,
                op0=MULT,
                op1=ADD,
            )
            lo = hi

        def mask_tables(j):
            nc.scalar.activation(
                out=rope_k[:, :, j, :], in_=rope_q[:, :, j, :], func=COPY, scale=mask_f32[:, j : j + 1]
            )

        for first in range(0, len(units) - UNITS_PER_ROUND, UNITS_PER_ROUND):
            for i in range(first, first + UNITS_PER_ROUND):
                rotate(units[i], turn_back(biased_of[i]))
            for i in range(first + HEAD_UNITS, min(first + HEAD_UNITS + UNITS_PER_ROUND, len(units))):
                biased_of[i] = project(units[i])
            this_round = first // UNITS_PER_ROUND
            if 1 <= this_round <= TILES // 2:
                mask_tables(2 * this_round - 2)
                mask_tables(2 * this_round - 1)

        last = [len(units) - 2, len(units) - 1]
        last_banks = [turn_back(biased_of[i]) for i in last]
        first_acc = project_v(HEAD_V_TILES)
        rotate(units[last[0]], last_banks[0])
        finish_v(HEAD_V_TILES, first_acc)
        second_acc = project_v(HEAD_V_TILES + 1)
        rotate(units[last[1]], last_banks[1])
        finish_v(HEAD_V_TILES + 1, second_acc)
        for j in range(HEAD_V_TILES + 2, TILES):
            finish_v(j, project_v(j))
